import numpy as np
import ml_dtypes


def mxq(x, axis, fmt="e4m3"):
    dtype, down = {"e4m3": (ml_dtypes.float8_e4m3fn, 7), "e5m2": (ml_dtypes.float8_e5m2, 14)}[fmt]
    v = np.moveaxis(np.asarray(x, np.float32).astype(ml_dtypes.bfloat16).astype(np.float64), axis, -1)
    blocks = v.reshape(v.shape[:-1] + (-1, 32))
    amax = np.abs(blocks).max(-1, keepdims=True)
    byte = np.maximum(np.where(amax > 0, np.frexp(amax)[1] - 1 + 127, 0) - down, 1)
    scale = np.exp2(byte - 127.0)
    codes = (blocks / scale).astype(np.float32).astype(dtype).astype(np.float64)
    return np.moveaxis((codes * scale).reshape(v.shape), -1, axis)


WIDE = False


def mx_kscale(k):
    if not WIDE:
        return np.ones(k)
    levels = np.array([10, -10, 5, -5, 0])
    a = np.random.permutation(np.resize(levels, k // 512 * 4)).reshape(k // 512, 4)
    idx = np.arange(k)
    return np.exp2(a[idx // 512, idx % 128 // 32])


BF16 = ml_dtypes.bfloat16


def bf(x):
    return np.asarray(x, np.float32).astype(BF16)


def f64(x):
    return np.asarray(x).astype(np.float64)


B, T, D, N, R = 2, 128, 512, 16384, 32

MAX_ATTENTION_SCALE = 1.0
MIN_ATTENTION_SCALE = 0.05
SCALE_GROWTH_RATE = 0.02
G = 4.0
C0 = 12.0


def cloud(rows, u):
    z = np.random.standard_normal((rows, R))
    return (z @ u / np.sqrt(R) + np.random.standard_normal((rows, D))) * (G / np.sqrt(2.0 * D))


def setup_inputs():
    t = mx_kscale(N)
    u = np.random.standard_normal((R, D))
    x = cloud(B * T, u).reshape(B, T, D)
    positions = cloud(N, u)
    c = C0 * (1.0 + 0.03 * np.random.standard_normal(N)) - np.log(t)
    sign = np.where(np.random.standard_normal(N) < 0.0, -1.0, 1.0)
    temperature = sign * (np.sqrt(2.0) * G / c / MIN_ATTENTION_SCALE - 0.1)
    values = np.random.standard_normal((N, D)) * 0.15 * np.sqrt(N) * (t.mean() / t)[:, None]
    return {"x": bf(x), "positions": bf(positions), "values": bf(values), "temperature": bf(temperature)}


def reference(x, positions, values, temperature):
    x, positions, values, temperature = f64(x), f64(positions), f64(values), f64(temperature)
    Bb, Tt, Dd = x.shape
    ages = np.zeros((positions.shape[0],))
    attention_scale = MIN_ATTENTION_SCALE + (MAX_ATTENTION_SCALE - MIN_ATTENTION_SCALE) * (1.0 - np.exp(-SCALE_GROWTH_RATE * ages))
    x_flat = x.reshape(-1, Dd)
    x2 = np.sum(x_flat * x_flat, axis=-1, keepdims=True)
    p2 = np.sum(positions * positions, axis=-1)[None, :]
    sq = x2 + p2 - 2.0 * (mxq(x_flat, 1, "e4m3") @ mxq(positions, 1, "e4m3").T)
    dists = np.sqrt(np.maximum(sq, 0.0))
    effective_temp = (np.abs(temperature) + 0.1) * attention_scale
    weights = np.exp(-dists / effective_temp[None, :])
    weights = weights / (np.sum(weights, axis=-1, keepdims=True) + 1e-8)
    out = mxq(weights, 1, "e4m3") @ mxq(values, 0, "e4m3")
    return out.reshape(Bb, Tt, Dd)

@@ -1,0 +1,271 @@
+import math
+from contextlib import ExitStack
+
+import concourse.mybir as mybir
+from concourse.masks import make_identity
+
+F32 = mybir.dt.float32
+BF16 = mybir.dt.bfloat16
+U32 = mybir.dt.uint32
+U8 = mybir.dt.uint8
+FP8X4 = mybir.dt.float8_e4m3fn_x4
+ALU = mybir.AluOpType
+ACT = mybir.ActivationFunctionType
+
+P = 128
+PACK = 4
+ROWS = 256
+HALVES = ROWS // P
+FEATURES = 512
+WORDS = FEATURES // 2
+ANCHORS = 16384
+CHUNK = P * PACK
+N_CHUNKS = ANCHORS // CHUNK
+ROUND = 8
+VECTOR_NORM_BLOCKS = 1
+
+FLOPS = 2 * 2 * ROWS * ANCHORS * FEATURES
+
+
+def transpose_words(nc, bank, rows_bf16, identity):
+    words = rows_bf16.bitcast(F32)
+    for u in range(WORDS // P):
+        nc.tensor.transpose(bank[:, u, :], words[:, u * P : (u + 1) * P], identity)
+
+
+def tile_multiscalegeometricattention_k_kernel(tc, x, positions, values, temperature, out):
+    nc = tc.nc
+    with ExitStack() as stack:
+        const = stack.enter_context(tc.tile_pool(name="const", bufs=1))
+        weights = stack.enter_context(tc.tile_pool(name="weights", bufs=1))
+        loads = stack.enter_context(tc.tile_pool(name="loads", bufs=3))
+        work = stack.enter_context(tc.tile_pool(name="work", bufs=2))
+        stats = stack.enter_context(tc.tile_pool(name="stats", bufs=4))
+        psum_misc = stack.enter_context(tc.psum_pool(name="psum_misc", bufs=1))
+        psum_t = stack.enter_context(tc.psum_pool(name="psum_t", bufs=3))
+        psum_s = stack.enter_context(tc.psum_pool(name="psum_s", bufs=2))
+        psum_o = stack.enter_context(tc.psum_pool(name="psum_o", bufs=1))
+
+        identity = const.tile([P, P], F32)
+        make_identity(nc, identity[:])
+        ones = const.tile([P, P], F32)
+        nc.vector.memset(ones[:], 1.0)
+        partial_sums = const.tile([P, PACK, ROWS], F32)
+        nc.gpsimd.memset(partial_sums[:], 0.0)
+
+        x_raw = const.tile([P, HALVES, FEATURES], BF16)
+        nc.sync.dma_start(out=x_raw[:], in_=x.rearrange("h r k -> r h k"))
+        temp_raw = const.tile([P, N_CHUNKS, PACK], BF16)
+        with nc.allow_non_contiguous_dma(reason="16,384 values, four to a piece"):
+            nc.sync.dma_start(
+                out=temp_raw[:], in_=temperature.rearrange("(c p j) -> p c j", p=P, j=PACK)
+            )
+
+        x_half_norm = const.tile([P, HALVES], F32)
+        for h in range(HALVES):
+            squares = stats.tile([P, FEATURES], BF16, tag="squares")
+            nc.scalar.activation(
+                out=squares[:],
+                in_=x_raw[:, h, :],
+                func=ACT.Square,
+                scale=math.sqrt(0.5),
+                accum_out=x_half_norm[:, h : h + 1],
+            )
+        x_t = psum_misc.tile([P, HALVES, WORDS // P, P], F32, tag="misc")
+        for h in range(HALVES):
+            transpose_words(nc, x_t[:, h, :, :], x_raw[:, h, :], identity[:])
+        x_grouped = const.tile([P, HALVES, P, WORDS // P], F32, align_bytes=64)
+        nc.vector.tensor_copy(out=x_grouped[:], in_=x_t[:].rearrange("q h u r -> q h r u"))
+        x_codes = const.tile([P, ROWS], U32, align_bytes=64)
+        x_scales = const.tile([P, ROWS], U8, align_bytes=64)
+        nc.vector.quantize_mx(
+            out=x_codes[:].bitcast(FP8X4),
+            scales=x_scales[:],
+            in_=x_grouped[:].rearrange("q h r u -> q (h r u)").bitcast(BF16),
+        )
+        spread = psum_misc.tile([P, HALVES, P], F32, tag="misc")
+        for h in range(HALVES):
+            nc.tensor.matmul(
+                out=spread[:, h, :],
+                lhsT=x_half_norm[:, h : h + 1].to_broadcast([P, P]),
+                rhs=identity[:],
+                start=True,
+                stop=True,
+            )
+        x_half_norm_rows = const.tile([P, ROWS], F32)
+        nc.vector.tensor_copy(out=x_half_norm_rows[:], in_=spread[:].rearrange("p h r -> p (h r)"))
+
+        n_blocks = N_CHUNKS * PACK
+        temp_flat = temp_raw[:].rearrange("p c j -> p (c j)")
+        negated = const.tile([P, n_blocks], F32)
+        nc.vector.tensor_scalar_mul(out=negated[:], in0=temp_flat, scalar1=-1.0)
+        tau = const.tile([P, n_blocks], F32)
+        nc.vector.tensor_tensor(out=tau[:], in0=temp_flat, in1=negated[:], op=ALU.max)
+        nc.vector.tensor_scalar(
+            out=tau[:], in0=tau[:], scalar1=0.1, scalar2=0.05, op0=ALU.add, op1=ALU.mult
+        )
+        minus_two_over_tau2 = const.tile([P, n_blocks], F32)
+        nc.vector.tensor_tensor(out=minus_two_over_tau2[:], in0=tau[:], in1=tau[:], op=ALU.mult)
+        nc.vector.reciprocal(out=minus_two_over_tau2[:], in_=minus_two_over_tau2[:])
+        nc.vector.tensor_scalar_mul(
+            out=minus_two_over_tau2[:], in0=minus_two_over_tau2[:], scalar1=-2.0
+        )
+
+        exps = [weights.tile([P, PACK, ROWS], F32, name="exps%d" % c) for c in range(N_CHUNKS)]
+
+        for first in range(0, N_CHUNKS, ROUND):
+            chunks_of_round = range(first, first + ROUND)
+            for c in chunks_of_round:
+                pos_raw = loads.tile([P, PACK, FEATURES], BF16)
+                nc.sync.dma_start(
+                    out=pos_raw[:],
+                    in_=positions[c * CHUNK : (c + 1) * CHUNK, :].rearrange("(p j) k -> p j k", j=PACK),
+                )
+
+                norm_scalar = stats.tile([P, PACK], F32)
+                norm_vector = stats.tile([P, PACK], F32)
+                half_norm = []
+                for j in range(PACK):
+                    if j < PACK - VECTOR_NORM_BLOCKS:
+                        squares = stats.tile([P, FEATURES], BF16, tag="squares")
+                        nc.scalar.activation(
+                            out=squares[:],
+                            in_=pos_raw[:, j, :],
+                            func=ACT.Square,
+                            scale=math.sqrt(0.5),
+                            accum_out=norm_scalar[:, j : j + 1],
+                        )
+                        half_norm.append(norm_scalar[:, j : j + 1])
+                    else:
+                        products = stats.tile([P, FEATURES], F32, tag="products", bufs=2)
+                        nc.vector.scalar_tensor_tensor(
+                            out=products[:],
+                            in0=pos_raw[:, j, :],
+                            scalar=0.5,
+                            in1=pos_raw[:, j, :],
+                            op0=ALU.mult,
+                            op1=ALU.mult,
+                            accum_out=norm_vector[:, j : j + 1],
+                        )
+                        half_norm.append(norm_vector[:, j : j + 1])
+
+                pos_grouped = work.tile([P, PACK, P, WORDS // P], F32, align_bytes=64)
+                for pair in range(PACK // 2):
+                    pos_t = psum_t.tile([P, 2, WORDS // P, P], F32)
+                    for b in range(2):
+                        transpose_words(nc, pos_t[:, b, :, :], pos_raw[:, 2 * pair + b, :], identity[:])
+                    nc.vector.tensor_copy(
+                        out=pos_grouped[:, 2 * pair : 2 * pair + 2, :, :],
+                        in_=pos_t[:].rearrange("q b u a -> q b a u"),
+                    )
+                pos_codes = work.tile([P, CHUNK], U32, align_bytes=64)
+                pos_scales = work.tile([P, CHUNK], U8, align_bytes=64)
+                nc.vector.quantize_mx(
+                    out=pos_codes[:].bitcast(FP8X4),
+                    scales=pos_scales[:],
+                    in_=pos_grouped[:].rearrange("q j a u -> q (j a u)").bitcast(BF16),
+                )
+
+                for pair in range(PACK // 2):
+                    dots = psum_s.tile([P, 2, ROWS], F32)
+                    for b in range(2):
+                        j = 2 * pair + b
+                        nc.tensor.matmul_mx(
+                            out=dots[:, b, :],
+                            lhsT=pos_codes[:, j * P : (j + 1) * P].bitcast(FP8X4),
+                            lhsT_scale=pos_scales[:, j * P : (j + 1) * P],
+                            rhs=x_codes[:].bitcast(FP8X4),
+                            rhs_scale=x_scales[:],
+                            start=True,
+                            stop=True,
+                        )
+                    for b in range(2):
+                        j = 2 * pair + b
+                        block = exps[c][:, j, :]
+                        nc.vector.scalar_tensor_tensor(
+                            out=block,
+                            in0=dots[:, b, :],
+                            scalar=half_norm[j],
+                            in1=x_half_norm_rows[:],
+                            op0=ALU.subtract,
+                            op1=ALU.subtract,
+                        )
+                        nc.vector.tensor_scalar(
+                            out=block,
+                            in0=block,
+                            scalar1=0.0,
+                            scalar2=minus_two_over_tau2[:, c * PACK + j : c * PACK + j + 1],
+                            op0=ALU.min,
+                            op1=ALU.mult,
+                        )
+
+            for c in chunks_of_round:
+                nc.scalar.activation(out=exps[c][:], in_=exps[c][:], func=ACT.Sqrt)
+            for c in chunks_of_round:
+                nc.scalar.activation(out=exps[c][:], in_=exps[c][:], func=ACT.Exp, scale=-1.0)
+                nc.gpsimd.tensor_tensor(
+                    out=partial_sums[:], in0=partial_sums[:], in1=exps[c][:], op=ALU.add
+                )
+
+        row_sums = psum_misc.tile([P, ROWS], F32, tag="misc")
+        for j in range(PACK):
+            nc.tensor.matmul(
+                out=row_sums[:],
+                lhsT=ones[:],
+                rhs=partial_sums[:, j, :],
+                start=(j == 0),
+                stop=(j == PACK - 1),
+            )
+        inverse_sums = const.tile([P, ROWS], F32)
+        nc.vector.tensor_scalar_add(out=inverse_sums[:], in0=row_sums[:], scalar1=1e-8)
+        nc.vector.reciprocal(out=inverse_sums[:], in_=inverse_sums[:])
+
+        sums = [psum_o.tile([P, FEATURES], F32, name="sums%d" % h) for h in range(HALVES)]
+        for c in range(N_CHUNKS):
+            val_raw = loads.tile([P, PACK, FEATURES], BF16)
+            nc.sync.dma_start(
+                out=val_raw[:],
+                in_=values[c * CHUNK : (c + 1) * CHUNK, :].rearrange("(p j) d -> p j d", j=PACK),
+            )
+            val_grouped = work.tile([P, FEATURES, PACK], BF16, align_bytes=64)
+            nc.scalar.copy(
+                out=val_grouped[:].rearrange("p (g i) j -> p g j i", i=4),
+                in_=val_raw[:].rearrange("p j (g i) -> p g j i", i=4),
+            )
+            val_codes = work.tile([P, FEATURES], U32, align_bytes=64)
+            val_scales = work.tile([P, FEATURES], U8, align_bytes=64)
+            nc.vector.quantize_mx(
+                out=val_codes[:].bitcast(FP8X4),
+                scales=val_scales[:],
+                in_=val_grouped[:].rearrange("p d j -> p (d j)"),
+            )
+
+            w_grouped = work.tile([P, ROWS, PACK], BF16, align_bytes=64)
+            nc.vector.tensor_tensor(
+                out=w_grouped[:],
+                in0=exps[c][:].rearrange("p j r -> p r j"),
+                in1=inverse_sums[:].unsqueeze(2).to_broadcast([P, ROWS, PACK]),
+                op=ALU.mult,
+            )
+            w_codes = work.tile([P, ROWS], U32, align_bytes=64)
+            w_scales = work.tile([P, ROWS], U8, align_bytes=64)
+            nc.vector.quantize_mx(
+                out=w_codes[:].bitcast(FP8X4),
+                scales=w_scales[:],
+                in_=w_grouped[:].rearrange("p r j -> p (r j)"),
+            )
+            for h in range(HALVES):
+                nc.tensor.matmul_mx(
+                    out=sums[h][:],
+                    lhsT=w_codes[:, h * P : (h + 1) * P].bitcast(FP8X4),
+                    lhsT_scale=w_scales[:, h * P : (h + 1) * P],
+                    rhs=val_codes[:].bitcast(FP8X4),
+                    rhs_scale=val_scales[:],
+                    start=(c == 0),
+                    stop=(c == N_CHUNKS - 1),
+                )
+
+        for h in range(HALVES):
+            result = work.tile([P, FEATURES], F32)
+            nc.vector.tensor_copy(out=result[:], in_=sums[h][:])
+            nc.sync.dma_start(out=out[h], in_=result[:])

@@ -18,31 +18,46 @@ ROWS = 256
 HALVES = ROWS // P
 FEATURES = 512
 WORDS = FEATURES // 2
+PLANES = WORDS // P
 ANCHORS = 16384
 CHUNK = P * PACK
 N_CHUNKS = ANCHORS // CHUNK
 ROUND = 8
 VECTOR_NORM_BLOCKS = 1
+VECTOR_SUM_CHUNKS = 4
+EARLY_EVERY = 4
+N_EARLY = N_CHUNKS // EARLY_EVERY
+RAW_BUFS = 4
 
 FLOPS = 2 * 2 * ROWS * ANCHORS * FEATURES
 
 
+def valid(c):
+    return 0 <= c < N_CHUNKS
+
+
+def late(c):
+    return valid(c) and c % EARLY_EVERY != 0
+
+
 def transpose_words(nc, bank, rows_bf16, identity):
     words = rows_bf16.bitcast(F32)
-    for u in range(WORDS // P):
+    for u in range(PLANES):
         nc.tensor.transpose(bank[:, u, :], words[:, u * P : (u + 1) * P], identity)
 
 
 def tile_multiscalegeometricattention_k_kernel(tc, x, positions, values, temperature, out):
     nc = tc.nc
     with ExitStack() as stack:
+        stack.enter_context(tc.manual_schedule())
         const = stack.enter_context(tc.tile_pool(name="const", bufs=1))
-        weights = stack.enter_context(tc.tile_pool(name="weights", bufs=1))
-        loads = stack.enter_context(tc.tile_pool(name="loads", bufs=3))
-        work = stack.enter_context(tc.tile_pool(name="work", bufs=2))
-        stats = stack.enter_context(tc.tile_pool(name="stats", bufs=4))
+        raw = stack.enter_context(tc.tile_pool(name="raw", bufs=RAW_BUFS))
+        grouped = stack.enter_context(tc.tile_pool(name="grouped", bufs=3))
+        packed = stack.enter_context(tc.tile_pool(name="packed", bufs=2))
+        late_packed = stack.enter_context(tc.tile_pool(name="late_packed", bufs=3))
+        scratch = stack.enter_context(tc.tile_pool(name="scratch", bufs=4))
         psum_misc = stack.enter_context(tc.psum_pool(name="psum_misc", bufs=1))
-        psum_t = stack.enter_context(tc.psum_pool(name="psum_t", bufs=3))
+        psum_t = stack.enter_context(tc.psum_pool(name="psum_t", bufs=2))
         psum_s = stack.enter_context(tc.psum_pool(name="psum_s", bufs=2))
         psum_o = stack.enter_context(tc.psum_pool(name="psum_o", bufs=1))
 
@@ -50,20 +65,22 @@ def tile_multiscalegeometricattention_k_kernel(tc, x, positions, values, tempera
         make_identity(nc, identity[:])
         ones = const.tile([P, P], F32)
         nc.vector.memset(ones[:], 1.0)
-        partial_sums = const.tile([P, PACK, ROWS], F32)
-        nc.gpsimd.memset(partial_sums[:], 0.0)
+        gpsimd_sums = const.tile([P, PACK, ROWS], F32)
+        nc.gpsimd.memset(gpsimd_sums[:], 0.0)
+        vector_sums = const.tile([P, PACK, ROWS], F32)
+        nc.vector.memset(vector_sums[:], 0.0)
 
         x_raw = const.tile([P, HALVES, FEATURES], BF16)
         nc.sync.dma_start(out=x_raw[:], in_=x.rearrange("h r k -> r h k"))
         temp_raw = const.tile([P, N_CHUNKS, PACK], BF16)
         with nc.allow_non_contiguous_dma(reason="16,384 values, four to a piece"):
-            nc.sync.dma_start(
+            nc.scalar.dma_start(
                 out=temp_raw[:], in_=temperature.rearrange("(c p j) -> p c j", p=P, j=PACK)
             )
 
         x_half_norm = const.tile([P, HALVES], F32)
         for h in range(HALVES):
-            squares = stats.tile([P, FEATURES], BF16, tag="squares")
+            squares = scratch.tile([P, FEATURES], BF16)
             nc.scalar.activation(
                 out=squares[:],
                 in_=x_raw[:, h, :],
@@ -71,10 +88,10 @@ def tile_multiscalegeometricattention_k_kernel(tc, x, positions, values, tempera
                 scale=math.sqrt(0.5),
                 accum_out=x_half_norm[:, h : h + 1],
             )
-        x_t = psum_misc.tile([P, HALVES, WORDS // P, P], F32, tag="misc")
+        x_t = psum_misc.tile([P, HALVES, PLANES, P], F32, tag="misc")
         for h in range(HALVES):
             transpose_words(nc, x_t[:, h, :, :], x_raw[:, h, :], identity[:])
-        x_grouped = const.tile([P, HALVES, P, WORDS // P], F32, align_bytes=64)
+        x_grouped = const.tile([P, HALVES, P, PLANES], F32, align_bytes=64)
         nc.vector.tensor_copy(out=x_grouped[:], in_=x_t[:].rearrange("q h u r -> q h r u"))
         x_codes = const.tile([P, ROWS], U32, align_bytes=64)
         x_scales = const.tile([P, ROWS], U8, align_bytes=64)
@@ -95,177 +112,259 @@ def tile_multiscalegeometricattention_k_kernel(tc, x, positions, values, tempera
         x_half_norm_rows = const.tile([P, ROWS], F32)
         nc.vector.tensor_copy(out=x_half_norm_rows[:], in_=spread[:].rearrange("p h r -> p (h r)"))
 
-        n_blocks = N_CHUNKS * PACK
+        exps = [const.tile([P, PACK, ROWS], F32, name="exps%d" % c) for c in range(N_CHUNKS)]
+        pos_raw, pos_t, pos_grouped, pos_codes, pos_scales, half_norm, dots = {}, {}, {}, {}, {}, {}, {}
+        val_raw, val_grouped, val_codes, val_scales = {}, {}, {}, {}
+        w_grouped, w_codes, w_scales = {}, {}, {}
+        minus_two_over_tau2 = const.tile([P, N_CHUNKS * PACK], F32)
+
+        def load_chunk(source, c):
+            chunk_raw = raw.tile([P, PACK, FEATURES], BF16)
+            nc.sync.dma_start(
+                out=chunk_raw[:],
+                in_=source[c * CHUNK : (c + 1) * CHUNK, :].rearrange("(p j) k -> p j k", j=PACK),
+            )
+            return chunk_raw
+
+        def transposes(c):
+            pos_t[c] = []
+            for pair in range(PACK // 2):
+                bank = psum_t.tile([P, 2, PLANES, P], F32)
+                for b in range(2):
+                    transpose_words(nc, bank[:, b, :, :], pos_raw[c][:, 2 * pair + b, :], identity[:])
+                pos_t[c].append(bank)
+
+        def norms(c):
+            norm_scalar = scratch.tile([P, PACK], F32)
+            norm_vector = scratch.tile([P, PACK], F32)
+            half_norm[c] = []
+            for j in range(PACK):
+                if j < PACK - VECTOR_NORM_BLOCKS:
+                    squares = scratch.tile([P, FEATURES], BF16)
+                    nc.scalar.activation(
+                        out=squares[:],
+                        in_=pos_raw[c][:, j, :],
+                        func=ACT.Square,
+                        scale=math.sqrt(0.5),
+                        accum_out=norm_scalar[:, j : j + 1],
+                    )
+                    half_norm[c].append(norm_scalar[:, j : j + 1])
+                else:
+                    products = scratch.tile([P, FEATURES], F32, bufs=2)
+                    nc.vector.scalar_tensor_tensor(
+                        out=products[:],
+                        in0=pos_raw[c][:, j, :],
+                        scalar=0.5,
+                        in1=pos_raw[c][:, j, :],
+                        op0=ALU.mult,
+                        op1=ALU.mult,
+                        accum_out=norm_vector[:, j : j + 1],
+                    )
+                    half_norm[c].append(norm_vector[:, j : j + 1])
+
+        def group_positions(c):
+            chunk_grouped = grouped.tile([P, PACK, P, PLANES], F32, tag="grouped", align_bytes=64)
+            for pair in range(PACK // 2):
+                nc.vector.tensor_copy(
+                    out=chunk_grouped[:, 2 * pair : 2 * pair + 2, :, :],
+                    in_=pos_t[c][pair][:].rearrange("q b u a -> q b a u"),
+                )
+            pos_grouped[c] = chunk_grouped
+
+        def quantise_positions(c):
+            codes = packed.tile([P, CHUNK], U32, tag="pos_codes", align_bytes=64)
+            scales = packed.tile([P, CHUNK], U8, tag="pos_scales", align_bytes=64)
+            nc.vector.quantize_mx(
+                out=codes[:].bitcast(FP8X4),
+                scales=scales[:],
+                in_=pos_grouped[c][:].rearrange("q j a u -> q (j a u)").bitcast(BF16),
+            )
+            pos_codes[c], pos_scales[c] = codes, scales
+
+        def first_passes(c):
+            dots[c] = []
+            for pair in range(PACK // 2):
+                bank = psum_s.tile([P, 2, ROWS], F32)
+                for b in range(2):
+                    j = 2 * pair + b
+                    nc.tensor.matmul_mx(
+                        out=bank[:, b, :],
+                        lhsT=pos_codes[c][:, j * P : (j + 1) * P].bitcast(FP8X4),
+                        lhsT_scale=pos_scales[c][:, j * P : (j + 1) * P],
+                        rhs=x_codes[:].bitcast(FP8X4),
+                        rhs_scale=x_scales[:],
+                        start=True,
+                        stop=True,
+                    )
+                dots[c].append(bank)
+
+        def arguments(c):
+            for j in range(PACK):
+                nc.vector.scalar_tensor_tensor(
+                    out=exps[c][:, j, :],
+                    in0=dots[c][j // 2][:, j % 2, :],
+                    scalar=half_norm[c][j],
+                    in1=x_half_norm_rows[:],
+                    op0=ALU.subtract,
+                    op1=ALU.subtract,
+                )
+            for j in range(PACK):
+                nc.vector.tensor_scalar(
+                    out=exps[c][:, j, :],
+                    in0=exps[c][:, j, :],
+                    scalar1=0.0,
+                    scalar2=minus_two_over_tau2[:, c * PACK + j : c * PACK + j + 1],
+                    op0=ALU.min,
+                    op1=ALU.mult,
+                )
+
+        def roots_and_exponentials(step):
+            place = step % ROUND
+            first = step - place - ROUND
+            if first < 0:
+                return
+            for c in (first + 2 * place % ROUND, first + 2 * place % ROUND + 1):
+                if place < ROUND // 2:
+                    nc.scalar.activation(out=exps[c][:], in_=exps[c][:], func=ACT.Sqrt)
+                else:
+                    nc.scalar.activation(out=exps[c][:], in_=exps[c][:], func=ACT.Exp, scale=-1.0)
+                    if c < N_CHUNKS - VECTOR_SUM_CHUNKS:
+                        nc.gpsimd.tensor_tensor(
+                            out=gpsimd_sums[:], in0=gpsimd_sums[:], in1=exps[c][:], op=ALU.add
+                        )
+                    else:
+                        nc.vector.tensor_tensor(
+                            out=vector_sums[:], in0=vector_sums[:], in1=exps[c][:], op=ALU.add
+                        )
+
+        def group_values(engine_copy, c):
+            chunk_grouped = grouped.tile([P, FEATURES, PACK], BF16, tag="grouped", align_bytes=64)
+            engine_copy(
+                out=chunk_grouped[:].rearrange("p (g i) j -> p g j i", i=4),
+                in_=val_raw[c][:].rearrange("p j (g i) -> p g j i", i=4),
+            )
+            val_grouped[c] = chunk_grouped
+
+        def quantise_values(pool, c):
+            codes = pool.tile([P, FEATURES], U32, tag="val_codes", align_bytes=64)
+            scales = pool.tile([P, FEATURES], U8, tag="val_scales", align_bytes=64)
+            nc.vector.quantize_mx(
+                out=codes[:].bitcast(FP8X4),
+                scales=scales[:],
+                in_=val_grouped[c][:].rearrange("p d j -> p (d j)"),
+            )
+            val_codes[c], val_scales[c] = codes, scales
+
+        early_packed = stack.enter_context(tc.tile_pool(name="early_packed", bufs=N_EARLY))
+        first_early_step = N_CHUNKS + ROUND - N_EARLY - VECTOR_SUM_CHUNKS // 2
+
+        def first_stage_step(step):
+            if valid(step + 6):
+                pos_raw[step + 6] = load_chunk(positions, step + 6)
+            e = step - first_early_step
+            if 0 <= e + 3 < N_EARLY:
+                val_raw[EARLY_EVERY * (e + 3)] = load_chunk(values, EARLY_EVERY * (e + 3))
+            if valid(step):
+                first_passes(step)
+            if valid(step + 2):
+                group_positions(step + 2)
+            if valid(step + 3):
+                transposes(step + 3)
+                norms(step + 3)
+            if valid(step + 1):
+                quantise_positions(step + 1)
+            if valid(step):
+                arguments(step)
+            if 0 <= e < N_EARLY:
+                group_values(nc.vector.tensor_copy, EARLY_EVERY * e)
+            if 0 <= e - 1 < N_EARLY:
+                quantise_values(early_packed, EARLY_EVERY * (e - 1))
+            roots_and_exponentials(step)
+
+        for step in range(-6, 0):
+            first_stage_step(step)
+
         temp_flat = temp_raw[:].rearrange("p c j -> p (c j)")
-        negated = const.tile([P, n_blocks], F32)
+        negated = const.tile([P, N_CHUNKS * PACK], F32)
         nc.vector.tensor_scalar_mul(out=negated[:], in0=temp_flat, scalar1=-1.0)
-        tau = const.tile([P, n_blocks], F32)
+        tau = const.tile([P, N_CHUNKS * PACK], F32)
         nc.vector.tensor_tensor(out=tau[:], in0=temp_flat, in1=negated[:], op=ALU.max)
         nc.vector.tensor_scalar(
             out=tau[:], in0=tau[:], scalar1=0.1, scalar2=0.05, op0=ALU.add, op1=ALU.mult
         )
-        minus_two_over_tau2 = const.tile([P, n_blocks], F32)
         nc.vector.tensor_tensor(out=minus_two_over_tau2[:], in0=tau[:], in1=tau[:], op=ALU.mult)
         nc.vector.reciprocal(out=minus_two_over_tau2[:], in_=minus_two_over_tau2[:])
         nc.vector.tensor_scalar_mul(
             out=minus_two_over_tau2[:], in0=minus_two_over_tau2[:], scalar1=-2.0
         )
 
-        exps = [weights.tile([P, PACK, ROWS], F32, name="exps%d" % c) for c in range(N_CHUNKS)]
-
-        for first in range(0, N_CHUNKS, ROUND):
-            chunks_of_round = range(first, first + ROUND)
-            for c in chunks_of_round:
-                pos_raw = loads.tile([P, PACK, FEATURES], BF16)
-                nc.sync.dma_start(
-                    out=pos_raw[:],
-                    in_=positions[c * CHUNK : (c + 1) * CHUNK, :].rearrange("(p j) k -> p j k", j=PACK),
-                )
-
-                norm_scalar = stats.tile([P, PACK], F32)
-                norm_vector = stats.tile([P, PACK], F32)
-                half_norm = []
-                for j in range(PACK):
-                    if j < PACK - VECTOR_NORM_BLOCKS:
-                        squares = stats.tile([P, FEATURES], BF16, tag="squares")
-                        nc.scalar.activation(
-                            out=squares[:],
-                            in_=pos_raw[:, j, :],
-                            func=ACT.Square,
-                            scale=math.sqrt(0.5),
-                            accum_out=norm_scalar[:, j : j + 1],
-                        )
-                        half_norm.append(norm_scalar[:, j : j + 1])
-                    else:
-                        products = stats.tile([P, FEATURES], F32, tag="products", bufs=2)
-                        nc.vector.scalar_tensor_tensor(
-                            out=products[:],
-                            in0=pos_raw[:, j, :],
-                            scalar=0.5,
-                            in1=pos_raw[:, j, :],
-                            op0=ALU.mult,
-                            op1=ALU.mult,
-                            accum_out=norm_vector[:, j : j + 1],
-                        )
-                        half_norm.append(norm_vector[:, j : j + 1])
-
-                pos_grouped = work.tile([P, PACK, P, WORDS // P], F32, align_bytes=64)
-                for pair in range(PACK // 2):
-                    pos_t = psum_t.tile([P, 2, WORDS // P, P], F32)
-                    for b in range(2):
-                        transpose_words(nc, pos_t[:, b, :, :], pos_raw[:, 2 * pair + b, :], identity[:])
-                    nc.vector.tensor_copy(
-                        out=pos_grouped[:, 2 * pair : 2 * pair + 2, :, :],
-                        in_=pos_t[:].rearrange("q b u a -> q b a u"),
-                    )
-                pos_codes = work.tile([P, CHUNK], U32, align_bytes=64)
-                pos_scales = work.tile([P, CHUNK], U8, align_bytes=64)
-                nc.vector.quantize_mx(
-                    out=pos_codes[:].bitcast(FP8X4),
-                    scales=pos_scales[:],
-                    in_=pos_grouped[:].rearrange("q j a u -> q (j a u)").bitcast(BF16),
-                )
-
-                for pair in range(PACK // 2):
-                    dots = psum_s.tile([P, 2, ROWS], F32)
-                    for b in range(2):
-                        j = 2 * pair + b
-                        nc.tensor.matmul_mx(
-                            out=dots[:, b, :],
-                            lhsT=pos_codes[:, j * P : (j + 1) * P].bitcast(FP8X4),
-                            lhsT_scale=pos_scales[:, j * P : (j + 1) * P],
-                            rhs=x_codes[:].bitcast(FP8X4),
-                            rhs_scale=x_scales[:],
-                            start=True,
-                            stop=True,
-                        )
-                    for b in range(2):
-                        j = 2 * pair + b
-                        block = exps[c][:, j, :]
-                        nc.vector.scalar_tensor_tensor(
-                            out=block,
-                            in0=dots[:, b, :],
-                            scalar=half_norm[j],
-                            in1=x_half_norm_rows[:],
-                            op0=ALU.subtract,
-                            op1=ALU.subtract,
-                        )
-                        nc.vector.tensor_scalar(
-                            out=block,
-                            in0=block,
-                            scalar1=0.0,
-                            scalar2=minus_two_over_tau2[:, c * PACK + j : c * PACK + j + 1],
-                            op0=ALU.min,
-                            op1=ALU.mult,
-                        )
-
-            for c in chunks_of_round:
-                nc.scalar.activation(out=exps[c][:], in_=exps[c][:], func=ACT.Sqrt)
-            for c in chunks_of_round:
-                nc.scalar.activation(out=exps[c][:], in_=exps[c][:], func=ACT.Exp, scale=-1.0)
-                nc.gpsimd.tensor_tensor(
-                    out=partial_sums[:], in0=partial_sums[:], in1=exps[c][:], op=ALU.add
-                )
+        for step in range(0, N_CHUNKS + ROUND):
+            first_stage_step(step)
 
         row_sums = psum_misc.tile([P, ROWS], F32, tag="misc")
         for j in range(PACK):
             nc.tensor.matmul(
-                out=row_sums[:],
-                lhsT=ones[:],
-                rhs=partial_sums[:, j, :],
-                start=(j == 0),
-                stop=(j == PACK - 1),
+                out=row_sums[:], lhsT=ones[:], rhs=gpsimd_sums[:, j, :], start=(j == 0), stop=False
+            )
+        for j in range(PACK):
+            nc.tensor.matmul(
+                out=row_sums[:], lhsT=ones[:], rhs=vector_sums[:, j, :], start=False, stop=(j == PACK - 1)
             )
         inverse_sums = const.tile([P, ROWS], F32)
         nc.vector.tensor_scalar_add(out=inverse_sums[:], in0=row_sums[:], scalar1=1e-8)
         nc.vector.reciprocal(out=inverse_sums[:], in_=inverse_sums[:])
 
         sums = [psum_o.tile([P, FEATURES], F32, name="sums%d" % h) for h in range(HALVES)]
-        for c in range(N_CHUNKS):
-            val_raw = loads.tile([P, PACK, FEATURES], BF16)
-            nc.sync.dma_start(
-                out=val_raw[:],
-                in_=values[c * CHUNK : (c + 1) * CHUNK, :].rearrange("(p j) d -> p j d", j=PACK),
-            )
-            val_grouped = work.tile([P, FEATURES, PACK], BF16, align_bytes=64)
-            nc.scalar.copy(
-                out=val_grouped[:].rearrange("p (g i) j -> p g j i", i=4),
-                in_=val_raw[:].rearrange("p j (g i) -> p g j i", i=4),
-            )
-            val_codes = work.tile([P, FEATURES], U32, align_bytes=64)
-            val_scales = work.tile([P, FEATURES], U8, align_bytes=64)
-            nc.vector.quantize_mx(
-                out=val_codes[:].bitcast(FP8X4),
-                scales=val_scales[:],
-                in_=val_grouped[:].rearrange("p d j -> p (d j)"),
-            )
 
-            w_grouped = work.tile([P, ROWS, PACK], BF16, align_bytes=64)
+        def normalise(c):
+            chunk_grouped = packed.tile([P, ROWS, PACK], BF16, tag="w_grouped", align_bytes=64)
             nc.vector.tensor_tensor(
-                out=w_grouped[:],
+                out=chunk_grouped[:],
                 in0=exps[c][:].rearrange("p j r -> p r j"),
                 in1=inverse_sums[:].unsqueeze(2).to_broadcast([P, ROWS, PACK]),
                 op=ALU.mult,
             )
-            w_codes = work.tile([P, ROWS], U32, align_bytes=64)
-            w_scales = work.tile([P, ROWS], U8, align_bytes=64)
+            w_grouped[c] = chunk_grouped
+
+        def quantise_weights(c):
+            codes = packed.tile([P, ROWS], U32, tag="w_codes", align_bytes=64)
+            scales = packed.tile([P, ROWS], U8, tag="w_scales", align_bytes=64)
             nc.vector.quantize_mx(
-                out=w_codes[:].bitcast(FP8X4),
-                scales=w_scales[:],
-                in_=w_grouped[:].rearrange("p r j -> p (r j)"),
+                out=codes[:].bitcast(FP8X4),
+                scales=scales[:],
+                in_=w_grouped[c][:].rearrange("p r j -> p (r j)"),
             )
+            w_codes[c], w_scales[c] = codes, scales
+
+        def second_passes(c):
             for h in range(HALVES):
                 nc.tensor.matmul_mx(
                     out=sums[h][:],
-                    lhsT=w_codes[:, h * P : (h + 1) * P].bitcast(FP8X4),
-                    lhsT_scale=w_scales[:, h * P : (h + 1) * P],
-                    rhs=val_codes[:].bitcast(FP8X4),
-                    rhs_scale=val_scales[:],
+                    lhsT=w_codes[c][:, h * P : (h + 1) * P].bitcast(FP8X4),
+                    lhsT_scale=w_scales[c][:, h * P : (h + 1) * P],
+                    rhs=val_codes[c][:].bitcast(FP8X4),
+                    rhs_scale=val_scales[c][:],
                     start=(c == 0),
                     stop=(c == N_CHUNKS - 1),
                 )
 
-        for h in range(HALVES):
-            result = work.tile([P, FEATURES], F32)
-            nc.vector.tensor_copy(out=result[:], in_=sums[h][:])
-            nc.sync.dma_start(out=out[h], in_=result[:])
+        for c in range(-6, N_CHUNKS):
+            if late(c + 6):
+                val_raw[c + 6] = load_chunk(values, c + 6)
+            if late(c + 3):
+                group_values(nc.scalar.copy, c + 3)
+            if valid(c + 1):
+                normalise(c + 1)
+            if valid(c):
+                quantise_weights(c)
+            if late(c + 2):
+                quantise_values(late_packed, c + 2)
+            if valid(c):
+                second_passes(c)
+
+        result_0 = grouped.tile([P, FEATURES], F32, tag="grouped", align_bytes=64)
+        nc.vector.tensor_copy(out=result_0[:], in_=sums[0][:])
+        nc.sync.dma_start(out=out[0], in_=result_0[:])
+        result_1 = grouped.tile([P, FEATURES], F32, tag="grouped", align_bytes=64)
+        nc.scalar.copy(out=result_1[:], in_=sums[1][:])
+        nc.scalar.dma_start(out=out[1], in_=result_1[:])

@@ -24,7 +24,7 @@ CHUNK = P * PACK
 N_CHUNKS = ANCHORS // CHUNK
 ROUND = 8
 VECTOR_NORM_BLOCKS = 1
-VECTOR_SUM_CHUNKS = 4
+SUM_LAG = ROUND + ROUND // 2 + 1
 EARLY_EVERY = 4
 N_EARLY = N_CHUNKS // EARLY_EVERY
 RAW_BUFS = 4
@@ -63,12 +63,8 @@ def tile_multiscalegeometricattention_k_kernel(tc, x, positions, values, tempera
 
         identity = const.tile([P, P], F32)
         make_identity(nc, identity[:])
-        ones = const.tile([P, P], F32)
+        ones = const.tile([P, 1], F32)
         nc.vector.memset(ones[:], 1.0)
-        gpsimd_sums = const.tile([P, PACK, ROWS], F32)
-        nc.gpsimd.memset(gpsimd_sums[:], 0.0)
-        vector_sums = const.tile([P, PACK, ROWS], F32)
-        nc.vector.memset(vector_sums[:], 0.0)
 
         x_raw = const.tile([P, HALVES, FEATURES], BF16)
         nc.sync.dma_start(out=x_raw[:], in_=x.rearrange("h r k -> r h k"))
@@ -221,21 +217,26 @@ def tile_multiscalegeometricattention_k_kernel(tc, x, positions, values, tempera
         def roots_and_exponentials(step):
             place = step % ROUND
             first = step - place - ROUND
-            if first < 0:
+            if not valid(first):
                 return
             for c in (first + 2 * place % ROUND, first + 2 * place % ROUND + 1):
                 if place < ROUND // 2:
                     nc.scalar.activation(out=exps[c][:], in_=exps[c][:], func=ACT.Sqrt)
                 else:
                     nc.scalar.activation(out=exps[c][:], in_=exps[c][:], func=ACT.Exp, scale=-1.0)
-                    if c < N_CHUNKS - VECTOR_SUM_CHUNKS:
-                        nc.gpsimd.tensor_tensor(
-                            out=gpsimd_sums[:], in0=gpsimd_sums[:], in1=exps[c][:], op=ALU.add
-                        )
-                    else:
-                        nc.vector.tensor_tensor(
-                            out=vector_sums[:], in0=vector_sums[:], in1=exps[c][:], op=ALU.add
-                        )
+
+        chunk_sums = psum_misc.tile([P, HALVES, N_CHUNKS], F32, tag="misc")
+
+        def add_to_row_sums(c):
+            for h in range(HALVES):
+                for j in range(PACK):
+                    nc.tensor.matmul(
+                        out=chunk_sums[:, h, c : c + 1],
+                        lhsT=exps[c][:, j, h * P : (h + 1) * P],
+                        rhs=ones[:],
+                        start=(j == 0),
+                        stop=(j == PACK - 1),
+                    )
 
         def group_values(engine_copy, c):
             chunk_grouped = grouped.tile([P, FEATURES, PACK], BF16, tag="grouped", align_bytes=64)
@@ -256,7 +257,7 @@ def tile_multiscalegeometricattention_k_kernel(tc, x, positions, values, tempera
             val_codes[c], val_scales[c] = codes, scales
 
         early_packed = stack.enter_context(tc.tile_pool(name="early_packed", bufs=N_EARLY))
-        first_early_step = N_CHUNKS + ROUND - N_EARLY - VECTOR_SUM_CHUNKS // 2
+        first_early_step = N_CHUNKS
 
         def first_stage_step(step):
             if valid(step + 6):
@@ -280,6 +281,8 @@ def tile_multiscalegeometricattention_k_kernel(tc, x, positions, values, tempera
             if 0 <= e - 1 < N_EARLY:
                 quantise_values(early_packed, EARLY_EVERY * (e - 1))
             roots_and_exponentials(step)
+            if valid(step - SUM_LAG):
+                add_to_row_sums(step - SUM_LAG)
 
         for step in range(-6, 0):
             first_stage_step(step)
@@ -298,21 +301,26 @@ def tile_multiscalegeometricattention_k_kernel(tc, x, positions, values, tempera
             out=minus_two_over_tau2[:], in0=minus_two_over_tau2[:], scalar1=-2.0
         )
 
-        for step in range(0, N_CHUNKS + ROUND):
+        for step in range(0, N_CHUNKS + SUM_LAG):
             first_stage_step(step)
 
-        row_sums = psum_misc.tile([P, ROWS], F32, tag="misc")
-        for j in range(PACK):
+        inverse_sum = const.tile([P, HALVES], F32)
+        nc.vector.tensor_reduce(
+            out=inverse_sum[:], in_=chunk_sums[:], axis=mybir.AxisListType.X, op=ALU.add
+        )
+        nc.vector.tensor_scalar_add(out=inverse_sum[:], in0=inverse_sum[:], scalar1=1e-8)
+        nc.vector.reciprocal(out=inverse_sum[:], in_=inverse_sum[:])
+        spread_sums = psum_misc.tile([P, HALVES, P], F32, tag="misc")
+        for h in range(HALVES):
             nc.tensor.matmul(
-                out=row_sums[:], lhsT=ones[:], rhs=gpsimd_sums[:, j, :], start=(j == 0), stop=False
-            )
-        for j in range(PACK):
-            nc.tensor.matmul(
-                out=row_sums[:], lhsT=ones[:], rhs=vector_sums[:, j, :], start=False, stop=(j == PACK - 1)
+                out=spread_sums[:, h, :],
+                lhsT=inverse_sum[:, h : h + 1].to_broadcast([P, P]),
+                rhs=identity[:],
+                start=True,
+                stop=True,
             )
         inverse_sums = const.tile([P, ROWS], F32)
-        nc.vector.tensor_scalar_add(out=inverse_sums[:], in0=row_sums[:], scalar1=1e-8)
-        nc.vector.reciprocal(out=inverse_sums[:], in_=inverse_sums[:])
+        nc.vector.tensor_copy(out=inverse_sums[:], in_=spread_sums[:].rearrange("p h r -> p (h r)"))
 
         sums = [psum_o.tile([P, FEATURES], F32, name="sums%d" % h) for h in range(HALVES)]
 

@@ -63,8 +63,6 @@ def tile_multiscalegeometricattention_k_kernel(tc, x, positions, values, tempera
 
         identity = const.tile([P, P], F32)
         make_identity(nc, identity[:])
-        ones = const.tile([P, 1], F32)
-        nc.vector.memset(ones[:], 1.0)
 
         x_raw = const.tile([P, HALVES, FEATURES], BF16)
         nc.sync.dma_start(out=x_raw[:], in_=x.rearrange("h r k -> r h k"))
@@ -225,17 +223,18 @@ def tile_multiscalegeometricattention_k_kernel(tc, x, positions, values, tempera
                 else:
                     nc.scalar.activation(out=exps[c][:], in_=exps[c][:], func=ACT.Exp, scale=-1.0)
 
-        chunk_sums = psum_misc.tile([P, HALVES, N_CHUNKS], F32, tag="misc")
+        anchor_sums = [psum_o.tile([P, P], F32, tag="sums%d" % h, name="anchor_sums%d" % h) for h in range(HALVES)]
 
         def add_to_row_sums(c):
             for h in range(HALVES):
                 for j in range(PACK):
                     nc.tensor.matmul(
-                        out=chunk_sums[:, h, c : c + 1],
+                        out=anchor_sums[h][:],
                         lhsT=exps[c][:, j, h * P : (h + 1) * P],
-                        rhs=ones[:],
-                        start=(j == 0),
-                        stop=(j == PACK - 1),
+                        rhs=identity[:],
+                        is_transpose=True,
+                        start=(c == 0 and j == 0),
+                        stop=(c == N_CHUNKS - 1 and j == PACK - 1),
                     )
 
         def group_values(engine_copy, c):
@@ -305,9 +304,10 @@ def tile_multiscalegeometricattention_k_kernel(tc, x, positions, values, tempera
             first_stage_step(step)
 
         inverse_sum = const.tile([P, HALVES], F32)
-        nc.vector.tensor_reduce(
-            out=inverse_sum[:], in_=chunk_sums[:], axis=mybir.AxisListType.X, op=ALU.add
-        )
+        for h in range(HALVES):
+            nc.vector.tensor_reduce(
+                out=inverse_sum[:, h : h + 1], in_=anchor_sums[h][:], axis=mybir.AxisListType.X, op=ALU.add
+            )
         nc.vector.tensor_scalar_add(out=inverse_sum[:], in0=inverse_sum[:], scalar1=1e-8)
         nc.vector.reciprocal(out=inverse_sum[:], in_=inverse_sum[:])
         spread_sums = psum_misc.tile([P, HALVES, P], F32, tag="misc")
@@ -322,7 +322,7 @@ def tile_multiscalegeometricattention_k_kernel(tc, x, positions, values, tempera
         inverse_sums = const.tile([P, ROWS], F32)
         nc.vector.tensor_copy(out=inverse_sums[:], in_=spread_sums[:].rearrange("p h r -> p (h r)"))
 
-        sums = [psum_o.tile([P, FEATURES], F32, name="sums%d" % h) for h in range(HALVES)]
+        sums = [psum_o.tile([P, FEATURES], F32, tag="sums%d" % h, name="sums%d" % h) for h in range(HALVES)]
 
         def normalise(c):
             chunk_grouped = packed.tile([P, ROWS, PACK], BF16, tag="w_grouped", align_bytes=64)

@@ -23,10 +23,9 @@ ANCHORS = 16384
 CHUNK = P * PACK
 N_CHUNKS = ANCHORS // CHUNK
 ROUND = 8
-VECTOR_NORM_BLOCKS = 1
 SUM_LAG = ROUND + ROUND // 2 + 1
-EARLY_EVERY = 4
-N_EARLY = N_CHUNKS // EARLY_EVERY
+EARLY_EVERY = 3
+N_EARLY = (N_CHUNKS + EARLY_EVERY - 1) // EARLY_EVERY
 RAW_BUFS = 4
 
 FLOPS = 2 * 2 * ROWS * ANCHORS * FEATURES
@@ -38,6 +37,12 @@ def valid(c):
 
 def late(c):
     return valid(c) and c % EARLY_EVERY != 0
+
+
+def vector_norm_blocks(c):
+    if c < ROUND:
+        return 0
+    return 1 + c % 2
 
 
 def transpose_words(nc, bank, rows_bf16, identity):
@@ -129,20 +134,18 @@ def tile_multiscalegeometricattention_k_kernel(tc, x, positions, values, tempera
                 pos_t[c].append(bank)
 
         def norms(c):
-            norm_scalar = scratch.tile([P, PACK], F32)
-            norm_vector = scratch.tile([P, PACK], F32)
             half_norm[c] = []
             for j in range(PACK):
-                if j < PACK - VECTOR_NORM_BLOCKS:
+                block_norm = scratch.tile([P, 1], F32, bufs=4 * PACK)
+                if j < PACK - vector_norm_blocks(c):
                     squares = scratch.tile([P, FEATURES], BF16)
                     nc.scalar.activation(
                         out=squares[:],
                         in_=pos_raw[c][:, j, :],
                         func=ACT.Square,
                         scale=math.sqrt(0.5),
-                        accum_out=norm_scalar[:, j : j + 1],
+                        accum_out=block_norm[:],
                     )
-                    half_norm[c].append(norm_scalar[:, j : j + 1])
                 else:
                     products = scratch.tile([P, FEATURES], F32, bufs=2)
                     nc.vector.scalar_tensor_tensor(
@@ -152,9 +155,9 @@ def tile_multiscalegeometricattention_k_kernel(tc, x, positions, values, tempera
                         in1=pos_raw[c][:, j, :],
                         op0=ALU.mult,
                         op1=ALU.mult,
-                        accum_out=norm_vector[:, j : j + 1],
+                        accum_out=block_norm[:],
                     )
-                    half_norm[c].append(norm_vector[:, j : j + 1])
+                half_norm[c].append(block_norm)
 
         def group_positions(c):
             chunk_grouped = grouped.tile([P, PACK, P, PLANES], F32, tag="grouped", align_bytes=64)
@@ -197,7 +200,7 @@ def tile_multiscalegeometricattention_k_kernel(tc, x, positions, values, tempera
                 nc.vector.scalar_tensor_tensor(
                     out=exps[c][:, j, :],
                     in0=dots[c][j // 2][:, j % 2, :],
-                    scalar=half_norm[c][j],
+                    scalar=half_norm[c][j][:],
                     in1=x_half_norm_rows[:],
                     op0=ALU.subtract,
                     op1=ALU.subtract,
@@ -319,8 +322,7 @@ def tile_multiscalegeometricattention_k_kernel(tc, x, positions, values, tempera
                 start=True,
                 stop=True,
             )
-        inverse_sums = const.tile([P, ROWS], F32)
-        nc.vector.tensor_copy(out=inverse_sums[:], in_=spread_sums[:].rearrange("p h r -> p (h r)"))
+        inverse_sums = spread_sums[:].rearrange("p h r -> p (h r)")
 
         sums = [psum_o.tile([P, FEATURES], F32, tag="sums%d" % h, name="sums%d" % h) for h in range(HALVES)]
 
@@ -329,7 +331,7 @@ def tile_multiscalegeometricattention_k_kernel(tc, x, positions, values, tempera
             nc.vector.tensor_tensor(
                 out=chunk_grouped[:],
                 in0=exps[c][:].rearrange("p j r -> p r j"),
-                in1=inverse_sums[:].unsqueeze(2).to_broadcast([P, ROWS, PACK]),
+                in1=inverse_sums.unsqueeze(2).to_broadcast([P, ROWS, PACK]),
                 op=ALU.mult,
             )
             w_grouped[c] = chunk_grouped

@@ -329,9 +329,9 @@ def tile_multiscalegeometricattention_k_kernel(tc, x, positions, values, tempera
         def normalise(c):
             chunk_grouped = packed.tile([P, ROWS, PACK], BF16, tag="w_grouped", align_bytes=64)
             nc.vector.tensor_tensor(
-                out=chunk_grouped[:],
-                in0=exps[c][:].rearrange("p j r -> p r j"),
-                in1=inverse_sums.unsqueeze(2).to_broadcast([P, ROWS, PACK]),
+                out=chunk_grouped[:].rearrange("p (g i) j -> p g j i", i=2),
+                in0=exps[c][:].rearrange("p j (g i) -> p g j i", i=2),
+                in1=inverse_sums.rearrange("p (g i) -> p g i", i=2).unsqueeze(2).to_broadcast([P, ROWS // 2, PACK, 2]),
                 op=ALU.mult,
             )
             w_grouped[c] = chunk_grouped

@@ -22,10 +22,7 @@ PLANES = WORDS // P
 ANCHORS = 16384
 CHUNK = P * PACK
 N_CHUNKS = ANCHORS // CHUNK
-ROUND = 8
-SUM_LAG = ROUND + ROUND // 2 + 1
-EARLY_EVERY = 3
-N_EARLY = (N_CHUNKS + EARLY_EVERY - 1) // EARLY_EVERY
+N_LATE = 12
 RAW_BUFS = 4
 
 FLOPS = 2 * 2 * ROWS * ANCHORS * FEATURES
@@ -35,14 +32,16 @@ def valid(c):
     return 0 <= c < N_CHUNKS
 
 
-def late(c):
-    return valid(c) and c % EARLY_EVERY != 0
-
-
-def vector_norm_blocks(c):
-    if c < ROUND:
-        return 0
+def gram_blocks(c):
     return 1 + c % 2
+
+
+def is_late(c):
+    return c * N_LATE % N_CHUNKS >= N_CHUNKS - N_LATE
+
+
+LATE = [c for c in range(N_CHUNKS) if is_late(c)]
+EARLY = [c for c in range(N_CHUNKS) if not is_late(c)]
 
 
 def transpose_words(nc, bank, rows_bf16, identity):
@@ -59,27 +58,19 @@ def tile_multiscalegeometricattention_k_kernel(tc, x, positions, values, tempera
         raw = stack.enter_context(tc.tile_pool(name="raw", bufs=RAW_BUFS))
         grouped = stack.enter_context(tc.tile_pool(name="grouped", bufs=3))
         packed = stack.enter_context(tc.tile_pool(name="packed", bufs=2))
-        late_packed = stack.enter_context(tc.tile_pool(name="late_packed", bufs=3))
         scratch = stack.enter_context(tc.tile_pool(name="scratch", bufs=4))
-        psum_misc = stack.enter_context(tc.psum_pool(name="psum_misc", bufs=1))
+        psum_misc = stack.enter_context(tc.psum_pool(name="psum_misc", bufs=2))
         psum_t = stack.enter_context(tc.psum_pool(name="psum_t", bufs=2))
-        psum_s = stack.enter_context(tc.psum_pool(name="psum_s", bufs=2))
-        psum_o = stack.enter_context(tc.psum_pool(name="psum_o", bufs=1))
+        psum_s = stack.enter_context(tc.psum_pool(name="psum_s", bufs=4))
 
         identity = const.tile([P, P], F32)
         make_identity(nc, identity[:])
 
         x_raw = const.tile([P, HALVES, FEATURES], BF16)
         nc.sync.dma_start(out=x_raw[:], in_=x.rearrange("h r k -> r h k"))
-        temp_raw = const.tile([P, N_CHUNKS, PACK], BF16)
-        with nc.allow_non_contiguous_dma(reason="16,384 values, four to a piece"):
-            nc.scalar.dma_start(
-                out=temp_raw[:], in_=temperature.rearrange("(c p j) -> p c j", p=P, j=PACK)
-            )
-
         x_half_norm = const.tile([P, HALVES], F32)
         for h in range(HALVES):
-            squares = scratch.tile([P, FEATURES], BF16)
+            squares = scratch.tile([P, FEATURES], BF16, bufs=2)
             nc.scalar.activation(
                 out=squares[:],
                 in_=x_raw[:, h, :],
@@ -112,9 +103,11 @@ def tile_multiscalegeometricattention_k_kernel(tc, x, positions, values, tempera
         nc.vector.tensor_copy(out=x_half_norm_rows[:], in_=spread[:].rearrange("p h r -> p (h r)"))
 
         exps = [const.tile([P, PACK, ROWS], F32, name="exps%d" % c) for c in range(N_CHUNKS)]
-        pos_raw, pos_t, pos_grouped, pos_codes, pos_scales, half_norm, dots = {}, {}, {}, {}, {}, {}, {}
+        pos_raw, pos_t, pos_grouped, pos_codes, pos_scales, half_norm, gram_bank, dots = {}, {}, {}, {}, {}, {}, {}, {}
         val_raw, val_grouped, val_codes, val_scales = {}, {}, {}, {}
         w_grouped, w_codes, w_scales = {}, {}, {}
+        temp_raw = const.tile([P, N_CHUNKS, PACK], BF16)
+        magnitude = const.tile([P, N_CHUNKS * PACK], F32)
         minus_two_over_tau2 = const.tile([P, N_CHUNKS * PACK], F32)
 
         def load_chunk(source, c):
@@ -134,43 +127,59 @@ def tile_multiscalegeometricattention_k_kernel(tc, x, positions, values, tempera
                 pos_t[c].append(bank)
 
         def norms(c):
-            half_norm[c] = []
-            for j in range(PACK):
-                block_norm = scratch.tile([P, 1], F32, bufs=4 * PACK)
-                if j < PACK - vector_norm_blocks(c):
-                    squares = scratch.tile([P, FEATURES], BF16)
-                    nc.scalar.activation(
-                        out=squares[:],
-                        in_=pos_raw[c][:, j, :],
-                        func=ACT.Square,
-                        scale=math.sqrt(0.5),
-                        accum_out=block_norm[:],
+            half_norm[c] = [scratch.tile([P, 1], F32, bufs=6 * PACK, name="block_norm") for j in range(PACK)]
+            for j in range(gram_blocks(c), PACK):
+                squares = scratch.tile([P, FEATURES], BF16, bufs=2)
+                nc.scalar.activation(
+                    out=squares[:],
+                    in_=pos_raw[c][:, j, :],
+                    func=ACT.Square,
+                    scale=math.sqrt(0.5),
+                    accum_out=half_norm[c][j][:],
+                )
+
+        def gram(c):
+            bank = psum_misc.tile([P, 2, P], F32, tag="misc")
+            features = pos_grouped[c][:].rearrange("q j a u -> q (j a u)").bitcast(BF16)
+            features = features.rearrange("q (j a t) -> q j a t", j=PACK, t=PACK)
+            for j in range(gram_blocks(c)):
+                for t in range(PACK):
+                    nc.tensor.matmul(
+                        out=bank[:, j, :],
+                        lhsT=features[:, j, :, t],
+                        rhs=features[:, j, :, t],
+                        start=(t == 0),
+                        stop=(t == PACK - 1),
                     )
-                else:
-                    products = scratch.tile([P, FEATURES], F32, bufs=2)
-                    nc.vector.scalar_tensor_tensor(
-                        out=products[:],
-                        in0=pos_raw[c][:, j, :],
-                        scalar=0.5,
-                        in1=pos_raw[c][:, j, :],
-                        op0=ALU.mult,
-                        op1=ALU.mult,
-                        accum_out=block_norm[:],
-                    )
-                half_norm[c].append(block_norm)
+            gram_bank[c] = bank
+
+        def gram_norms(c):
+            for j in range(gram_blocks(c)):
+                diagonal = scratch.tile([P, P], F32, bufs=2)
+                nc.vector.scalar_tensor_tensor(
+                    out=diagonal[:],
+                    in0=gram_bank[c][:, j, :],
+                    scalar=0.5,
+                    in1=identity[:],
+                    op0=ALU.mult,
+                    op1=ALU.mult,
+                    accum_out=half_norm[c][j][:],
+                )
 
         def group_positions(c):
             chunk_grouped = grouped.tile([P, PACK, P, PLANES], F32, tag="grouped", align_bytes=64)
             for pair in range(PACK // 2):
-                nc.vector.tensor_copy(
+                on_scalar = c > 2 and (pair == 1 or c % 4 == 3)
+                engine_copy = nc.scalar.copy if on_scalar else nc.vector.tensor_copy
+                engine_copy(
                     out=chunk_grouped[:, 2 * pair : 2 * pair + 2, :, :],
                     in_=pos_t[c][pair][:].rearrange("q b u a -> q b a u"),
                 )
             pos_grouped[c] = chunk_grouped
 
         def quantise_positions(c):
-            codes = packed.tile([P, CHUNK], U32, tag="pos_codes", align_bytes=64)
-            scales = packed.tile([P, CHUNK], U8, tag="pos_scales", align_bytes=64)
+            codes = packed.tile([P, CHUNK], U32, tag="codes", bufs=3, align_bytes=64)
+            scales = packed.tile([P, CHUNK], U8, tag="scales", bufs=3, align_bytes=64)
             nc.vector.quantize_mx(
                 out=codes[:].bitcast(FP8X4),
                 scales=scales[:],
@@ -181,7 +190,7 @@ def tile_multiscalegeometricattention_k_kernel(tc, x, positions, values, tempera
         def first_passes(c):
             dots[c] = []
             for pair in range(PACK // 2):
-                bank = psum_s.tile([P, 2, ROWS], F32)
+                bank = psum_s.tile([P, 2, ROWS], F32, tag="bank")
                 for b in range(2):
                     j = 2 * pair + b
                     nc.tensor.matmul_mx(
@@ -195,7 +204,7 @@ def tile_multiscalegeometricattention_k_kernel(tc, x, positions, values, tempera
                     )
                 dots[c].append(bank)
 
-        def arguments(c):
+        def half_distances(c):
             for j in range(PACK):
                 nc.vector.scalar_tensor_tensor(
                     out=exps[c][:, j, :],
@@ -205,6 +214,8 @@ def tile_multiscalegeometricattention_k_kernel(tc, x, positions, values, tempera
                     op0=ALU.subtract,
                     op1=ALU.subtract,
                 )
+
+        def arguments(c):
             for j in range(PACK):
                 nc.vector.tensor_scalar(
                     out=exps[c][:, j, :],
@@ -215,29 +226,40 @@ def tile_multiscalegeometricattention_k_kernel(tc, x, positions, values, tempera
                     op1=ALU.mult,
                 )
 
-        def roots_and_exponentials(step):
-            place = step % ROUND
-            first = step - place - ROUND
-            if not valid(first):
-                return
-            for c in (first + 2 * place % ROUND, first + 2 * place % ROUND + 1):
-                if place < ROUND // 2:
-                    nc.scalar.activation(out=exps[c][:], in_=exps[c][:], func=ACT.Sqrt)
-                else:
-                    nc.scalar.activation(out=exps[c][:], in_=exps[c][:], func=ACT.Exp, scale=-1.0)
+        def inverse_temperatures():
+            shifted = const.tile([P, N_CHUNKS * PACK], F32)
+            nc.vector.tensor_scalar_add(out=shifted[:], in0=magnitude[:], scalar1=0.1)
+            nc.vector.scalar_tensor_tensor(
+                out=minus_two_over_tau2[:],
+                in0=shifted[:],
+                scalar=-1.0 / 800.0,
+                in1=shifted[:],
+                op0=ALU.mult,
+                op1=ALU.mult,
+            )
+            nc.vector.reciprocal(out=minus_two_over_tau2[:], in_=minus_two_over_tau2[:])
 
-        anchor_sums = [psum_o.tile([P, P], F32, tag="sums%d" % h, name="anchor_sums%d" % h) for h in range(HALVES)]
+        def temperature_magnitudes():
+            nc.scalar.activation(out=magnitude[:], in_=temp_raw[:].rearrange("p c j -> p (c j)"), func=ACT.Abs)
+
+        def root(c):
+            nc.scalar.activation(out=exps[c][:], in_=exps[c][:], func=ACT.Sqrt)
+
+        def exponential(c):
+            nc.scalar.activation(out=exps[c][:], in_=exps[c][:], func=ACT.Exp, scale=-1.0)
+
+        anchor_sums = []
 
         def add_to_row_sums(c):
             for h in range(HALVES):
                 for j in range(PACK):
                     nc.tensor.matmul(
-                        out=anchor_sums[h][:],
+                        out=anchor_sums[0][:, h, :],
                         lhsT=exps[c][:, j, h * P : (h + 1) * P],
                         rhs=identity[:],
                         is_transpose=True,
-                        start=(c == 0 and j == 0),
-                        stop=(c == N_CHUNKS - 1 and j == PACK - 1),
+                        start=(c == 0 and h == 0 and j == 0),
+                        stop=(c == N_CHUNKS - 1 and h == HALVES - 1 and j == PACK - 1),
                     )
 
         def group_values(engine_copy, c):
@@ -248,9 +270,9 @@ def tile_multiscalegeometricattention_k_kernel(tc, x, positions, values, tempera
             )
             val_grouped[c] = chunk_grouped
 
-        def quantise_values(pool, c):
-            codes = pool.tile([P, FEATURES], U32, tag="val_codes", align_bytes=64)
-            scales = pool.tile([P, FEATURES], U8, tag="val_scales", align_bytes=64)
+        def quantise_values(pool, bufs, c):
+            codes = pool.tile([P, FEATURES], U32, tag="codes", bufs=bufs, align_bytes=64)
+            scales = pool.tile([P, FEATURES], U8, tag="scales", bufs=bufs, align_bytes=64)
             nc.vector.quantize_mx(
                 out=codes[:].bitcast(FP8X4),
                 scales=scales[:],
@@ -258,62 +280,68 @@ def tile_multiscalegeometricattention_k_kernel(tc, x, positions, values, tempera
             )
             val_codes[c], val_scales[c] = codes, scales
 
-        early_packed = stack.enter_context(tc.tile_pool(name="early_packed", bufs=N_EARLY))
-        first_early_step = N_CHUNKS
+        early_packed = stack.enter_context(tc.tile_pool(name="early_packed", bufs=1))
 
         def first_stage_step(step):
-            if valid(step + 6):
-                pos_raw[step + 6] = load_chunk(positions, step + 6)
-            e = step - first_early_step
-            if 0 <= e + 3 < N_EARLY:
-                val_raw[EARLY_EVERY * (e + 3)] = load_chunk(values, EARLY_EVERY * (e + 3))
-            if valid(step):
-                first_passes(step)
-            if valid(step + 2):
-                group_positions(step + 2)
-            if valid(step + 3):
-                transposes(step + 3)
-                norms(step + 3)
+            if valid(step + 7):
+                pos_raw[step + 7] = load_chunk(positions, step + 7)
             if valid(step + 1):
-                quantise_positions(step + 1)
+                first_passes(step + 1)
+            if valid(step + 3):
+                group_positions(step + 3)
+            if valid(step + 4):
+                transposes(step + 4)
+                norms(step + 4)
+            if step == -3:
+                temperature_magnitudes()
+            if valid(step + 2):
+                gram(step + 2)
+            if valid(step):
+                half_distances(step)
+            if step == 0:
+                inverse_temperatures()
             if valid(step):
                 arguments(step)
-            if 0 <= e < N_EARLY:
-                group_values(nc.vector.tensor_copy, EARLY_EVERY * e)
-            if 0 <= e - 1 < N_EARLY:
-                quantise_values(early_packed, EARLY_EVERY * (e - 1))
-            roots_and_exponentials(step)
-            if valid(step - SUM_LAG):
-                add_to_row_sums(step - SUM_LAG)
+            if valid(step + 2):
+                quantise_positions(step + 2)
+            if valid(step + 1):
+                gram_norms(step + 1)
+            if valid(step - 1):
+                root(step - 1)
 
-        for step in range(-6, 0):
+        for step in range(-7, N_CHUNKS + 1):
             first_stage_step(step)
+            if step == -6:
+                with nc.allow_non_contiguous_dma(reason="16,384 values, four to a piece"):
+                    nc.sync.dma_start(
+                        out=temp_raw[:], in_=temperature.rearrange("(c p j) -> p c j", p=P, j=PACK)
+                    )
 
-        temp_flat = temp_raw[:].rearrange("p c j -> p (c j)")
-        negated = const.tile([P, N_CHUNKS * PACK], F32)
-        nc.vector.tensor_scalar_mul(out=negated[:], in0=temp_flat, scalar1=-1.0)
-        tau = const.tile([P, N_CHUNKS * PACK], F32)
-        nc.vector.tensor_tensor(out=tau[:], in0=temp_flat, in1=negated[:], op=ALU.max)
-        nc.vector.tensor_scalar(
-            out=tau[:], in0=tau[:], scalar1=0.1, scalar2=0.05, op0=ALU.add, op1=ALU.mult
-        )
-        nc.vector.tensor_tensor(out=minus_two_over_tau2[:], in0=tau[:], in1=tau[:], op=ALU.mult)
-        nc.vector.reciprocal(out=minus_two_over_tau2[:], in_=minus_two_over_tau2[:])
-        nc.vector.tensor_scalar_mul(
-            out=minus_two_over_tau2[:], in0=minus_two_over_tau2[:], scalar1=-2.0
-        )
+        anchor_sums.append(psum_s.tile([P, HALVES, P], F32, tag="bank", name="anchor_sums"))
+        order = EARLY + LATE
+        for c in order[:3]:
+            val_raw[c] = load_chunk(values, c)
+        for e in range(N_CHUNKS + 1):
+            if e < N_CHUNKS:
+                exponential(e)
+                add_to_row_sums(e)
+            if e < len(EARLY):
+                group_values(nc.vector.tensor_copy, EARLY[e])
+            if 0 <= e - 1 < len(EARLY):
+                quantise_values(early_packed, len(EARLY), EARLY[e - 1])
+            if e + 3 < len(EARLY) + 3:
+                val_raw[order[e + 3]] = load_chunk(values, order[e + 3])
 
-        for step in range(0, N_CHUNKS + SUM_LAG):
-            first_stage_step(step)
+        for i in range(2):
+            group_values(nc.scalar.copy, LATE[i])
 
         inverse_sum = const.tile([P, HALVES], F32)
-        for h in range(HALVES):
-            nc.vector.tensor_reduce(
-                out=inverse_sum[:, h : h + 1], in_=anchor_sums[h][:], axis=mybir.AxisListType.X, op=ALU.add
-            )
+        nc.vector.tensor_reduce(
+            out=inverse_sum[:], in_=anchor_sums[0][:], axis=mybir.AxisListType.X, op=ALU.add
+        )
         nc.vector.tensor_scalar_add(out=inverse_sum[:], in0=inverse_sum[:], scalar1=1e-8)
         nc.vector.reciprocal(out=inverse_sum[:], in_=inverse_sum[:])
-        spread_sums = psum_misc.tile([P, HALVES, P], F32, tag="misc")
+        spread_sums = psum_s.tile([P, HALVES, P], F32, tag="bank")
         for h in range(HALVES):
             nc.tensor.matmul(
                 out=spread_sums[:, h, :],
@@ -324,7 +352,9 @@ def tile_multiscalegeometricattention_k_kernel(tc, x, positions, values, tempera
             )
         inverse_sums = spread_sums[:].rearrange("p h r -> p (h r)")
 
-        sums = [psum_o.tile([P, FEATURES], F32, tag="sums%d" % h, name="sums%d" % h) for h in range(HALVES)]
+        quantise_values(packed, 3, LATE[0])
+
+        sums = [psum_s.tile([P, FEATURES], F32, tag="bank", name="sums%d" % h) for h in range(HALVES)]
 
         def normalise(c):
             chunk_grouped = packed.tile([P, ROWS, PACK], BF16, tag="w_grouped", align_bytes=64)
@@ -358,17 +388,19 @@ def tile_multiscalegeometricattention_k_kernel(tc, x, positions, values, tempera
                     stop=(c == N_CHUNKS - 1),
                 )
 
-        for c in range(-6, N_CHUNKS):
-            if late(c + 6):
-                val_raw[c + 6] = load_chunk(values, c + 6)
-            if late(c + 3):
-                group_values(nc.scalar.copy, c + 3)
+        for c in range(-1, N_CHUNKS):
             if valid(c + 1):
                 normalise(c + 1)
             if valid(c):
                 quantise_weights(c)
-            if late(c + 2):
-                quantise_values(late_packed, c + 2)
+            if c in LATE:
+                i = LATE.index(c)
+                if i + 3 < N_LATE:
+                    val_raw[LATE[i + 3]] = load_chunk(values, LATE[i + 3])
+                if i + 2 < N_LATE:
+                    group_values(nc.scalar.copy, LATE[i + 2])
+                if i + 1 < N_LATE:
+                    quantise_values(packed, 3, LATE[i + 1])
             if valid(c):
                 second_passes(c)
 

@@ -22,6 +22,7 @@ PLANES = WORDS // P
 ANCHORS = 16384
 CHUNK = P * PACK
 N_CHUNKS = ANCHORS // CHUNK
+POOL_ROWS = 64
 N_LATE = 12
 RAW_BUFS = 4
 
@@ -351,19 +352,27 @@ def tile_multiscalegeometricattention_k_kernel(tc, x, positions, values, tempera
                 stop=True,
             )
         inverse_sums = spread_sums[:].rearrange("p h r -> p (h r)")
+        pool_inverse_sums = const.tile([P, POOL_ROWS], F32)
+        nc.vector.tensor_copy(out=pool_inverse_sums[:], in_=inverse_sums[:, ROWS - POOL_ROWS :])
 
         quantise_values(packed, 3, LATE[0])
 
         sums = [psum_s.tile([P, FEATURES], F32, tag="bank", name="sums%d" % h) for h in range(HALVES)]
 
         def normalise(c):
-            chunk_grouped = packed.tile([P, ROWS, PACK], BF16, tag="w_grouped", align_bytes=64)
-            nc.vector.tensor_tensor(
-                out=chunk_grouped[:].rearrange("p (g i) j -> p g j i", i=2),
-                in0=exps[c][:].rearrange("p j (g i) -> p g j i", i=2),
-                in1=inverse_sums.rearrange("p (g i) -> p g i", i=2).unsqueeze(2).to_broadcast([P, ROWS // 2, PACK, 2]),
-                op=ALU.mult,
-            )
+            chunk_grouped = packed.tile([P, ROWS, PACK], BF16, tag="w_grouped", bufs=3, align_bytes=64)
+            vector_rows = ROWS - POOL_ROWS
+            for engine, rows, inverses in (
+                (nc.gpsimd, slice(vector_rows, ROWS), pool_inverse_sums[:]),
+                (nc.vector, slice(0, vector_rows), inverse_sums[:, :vector_rows]),
+            ):
+                pairs = (rows.stop - rows.start) // 2
+                engine.tensor_tensor(
+                    out=chunk_grouped[:, rows, :].rearrange("p (g i) j -> p g j i", i=2),
+                    in0=exps[c][:, :, rows].rearrange("p j (g i) -> p g j i", i=2),
+                    in1=inverses.rearrange("p (g i) -> p g i", i=2).unsqueeze(2).to_broadcast([P, pairs, PACK, 2]),
+                    op=ALU.mult,
+                )
             w_grouped[c] = chunk_grouped
 
         def quantise_weights(c):

@@ -22,8 +22,11 @@ PLANES = WORDS // P
 ANCHORS = 16384
 CHUNK = P * PACK
 N_CHUNKS = ANCHORS // CHUNK
-POOL_ROWS = 64
-N_LATE = 12
+POOL_ROWS = 40
+VECTOR_ROWS = P - POOL_ROWS
+N_LATE = 16
+N_FIRST = 12
+INVERSES_AT = N_CHUNKS - 4
 RAW_BUFS = 4
 
 FLOPS = 2 * 2 * ROWS * ANCHORS * FEATURES
@@ -38,7 +41,7 @@ def gram_blocks(c):
 
 
 def is_late(c):
-    return c * N_LATE % N_CHUNKS >= N_CHUNKS - N_LATE
+    return c * N_LATE % N_CHUNKS < N_LATE
 
 
 LATE = [c for c in range(N_CHUNKS) if is_late(c)]
@@ -67,7 +70,7 @@ def tile_multiscalegeometricattention_k_kernel(tc, x, positions, values, tempera
         identity = const.tile([P, P], F32)
         make_identity(nc, identity[:])
 
-        x_raw = const.tile([P, HALVES, FEATURES], BF16)
+        x_raw = raw.tile([P, HALVES, FEATURES], BF16, tag="chunk_raw")
         nc.sync.dma_start(out=x_raw[:], in_=x.rearrange("h r k -> r h k"))
         x_half_norm = const.tile([P, HALVES], F32)
         for h in range(HALVES):
@@ -82,7 +85,7 @@ def tile_multiscalegeometricattention_k_kernel(tc, x, positions, values, tempera
         x_t = psum_misc.tile([P, HALVES, PLANES, P], F32, tag="misc")
         for h in range(HALVES):
             transpose_words(nc, x_t[:, h, :, :], x_raw[:, h, :], identity[:])
-        x_grouped = const.tile([P, HALVES, P, PLANES], F32, align_bytes=64)
+        x_grouped = grouped.tile([P, HALVES, P, PLANES], F32, tag="grouped", align_bytes=64)
         nc.vector.tensor_copy(out=x_grouped[:], in_=x_t[:].rearrange("q h u r -> q h r u"))
         x_codes = const.tile([P, ROWS], U32, align_bytes=64)
         x_scales = const.tile([P, ROWS], U8, align_bytes=64)
@@ -112,7 +115,7 @@ def tile_multiscalegeometricattention_k_kernel(tc, x, positions, values, tempera
         minus_two_over_tau2 = const.tile([P, N_CHUNKS * PACK], F32)
 
         def load_chunk(source, c):
-            chunk_raw = raw.tile([P, PACK, FEATURES], BF16)
+            chunk_raw = raw.tile([P, PACK, FEATURES], BF16, tag="chunk_raw")
             nc.sync.dma_start(
                 out=chunk_raw[:],
                 in_=source[c * CHUNK : (c + 1) * CHUNK, :].rearrange("(p j) k -> p j k", j=PACK),
@@ -170,7 +173,7 @@ def tile_multiscalegeometricattention_k_kernel(tc, x, positions, values, tempera
         def group_positions(c):
             chunk_grouped = grouped.tile([P, PACK, P, PLANES], F32, tag="grouped", align_bytes=64)
             for pair in range(PACK // 2):
-                on_scalar = c > 2 and (pair == 1 or c % 4 == 3)
+                on_scalar = c > 2 and pair == 1
                 engine_copy = nc.scalar.copy if on_scalar else nc.vector.tensor_copy
                 engine_copy(
                     out=chunk_grouped[:, 2 * pair : 2 * pair + 2, :, :],
@@ -179,8 +182,8 @@ def tile_multiscalegeometricattention_k_kernel(tc, x, positions, values, tempera
             pos_grouped[c] = chunk_grouped
 
         def quantise_positions(c):
-            codes = packed.tile([P, CHUNK], U32, tag="codes", bufs=3, align_bytes=64)
-            scales = packed.tile([P, CHUNK], U8, tag="scales", bufs=3, align_bytes=64)
+            codes = packed.tile([P, CHUNK], U32, tag="codes", bufs=4, align_bytes=64)
+            scales = packed.tile([P, CHUNK], U8, tag="scales", bufs=4, align_bytes=64)
             nc.vector.quantize_mx(
                 out=codes[:].bitcast(FP8X4),
                 scales=scales[:],
@@ -228,13 +231,12 @@ def tile_multiscalegeometricattention_k_kernel(tc, x, positions, values, tempera
                 )
 
         def inverse_temperatures():
-            shifted = const.tile([P, N_CHUNKS * PACK], F32)
-            nc.vector.tensor_scalar_add(out=shifted[:], in0=magnitude[:], scalar1=0.1)
+            nc.vector.tensor_scalar_add(out=magnitude[:], in0=magnitude[:], scalar1=0.1)
             nc.vector.scalar_tensor_tensor(
                 out=minus_two_over_tau2[:],
-                in0=shifted[:],
+                in0=magnitude[:],
                 scalar=-1.0 / 800.0,
-                in1=shifted[:],
+                in1=magnitude[:],
                 op0=ALU.mult,
                 op1=ALU.mult,
             )
@@ -246,22 +248,23 @@ def tile_multiscalegeometricattention_k_kernel(tc, x, positions, values, tempera
         def root(c):
             nc.scalar.activation(out=exps[c][:], in_=exps[c][:], func=ACT.Sqrt)
 
-        def exponential(c):
-            nc.scalar.activation(out=exps[c][:], in_=exps[c][:], func=ACT.Exp, scale=-1.0)
+        def half_rows(h):
+            return slice(h * P, (h + 1) * P)
 
-        anchor_sums = []
+        def exponential(c, h):
+            half = exps[c][:, :, half_rows(h)]
+            nc.scalar.activation(out=half, in_=half, func=ACT.Exp, scale=-1.0)
 
-        def add_to_row_sums(c):
-            for h in range(HALVES):
-                for j in range(PACK):
-                    nc.tensor.matmul(
-                        out=anchor_sums[0][:, h, :],
-                        lhsT=exps[c][:, j, h * P : (h + 1) * P],
-                        rhs=identity[:],
-                        is_transpose=True,
-                        start=(c == 0 and h == 0 and j == 0),
-                        stop=(c == N_CHUNKS - 1 and h == HALVES - 1 and j == PACK - 1),
-                    )
+        def add_to_row_sums(c, h):
+            for j in range(PACK):
+                nc.tensor.matmul(
+                    out=anchor_sums[h][:],
+                    lhsT=exps[c][:, j, half_rows(h)],
+                    rhs=identity[:],
+                    is_transpose=True,
+                    start=(c == 0 and j == 0),
+                    stop=(c == N_CHUNKS - 1 and j == PACK - 1),
+                )
 
         def group_values(engine_copy, c):
             chunk_grouped = grouped.tile([P, FEATURES, PACK], BF16, tag="grouped", align_bytes=64)
@@ -318,104 +321,120 @@ def tile_multiscalegeometricattention_k_kernel(tc, x, positions, values, tempera
                         out=temp_raw[:], in_=temperature.rearrange("(c p j) -> p c j", p=P, j=PACK)
                     )
 
-        anchor_sums.append(psum_s.tile([P, HALVES, P], F32, tag="bank", name="anchor_sums"))
+        anchor_sums = [psum_s.tile([P, P], F32, tag="bank", name="anchor_sums%d" % h) for h in range(HALVES)]
         order = EARLY + LATE
-        for c in order[:3]:
-            val_raw[c] = load_chunk(values, c)
-        for e in range(N_CHUNKS + 1):
-            if e < N_CHUNKS:
-                exponential(e)
-                add_to_row_sums(e)
-            if e < len(EARLY):
-                group_values(nc.vector.tensor_copy, EARLY[e])
-            if 0 <= e - 1 < len(EARLY):
-                quantise_values(early_packed, len(EARLY), EARLY[e - 1])
-            if e + 3 < len(EARLY) + 3:
-                val_raw[order[e + 3]] = load_chunk(values, order[e + 3])
 
-        for i in range(2):
-            group_values(nc.scalar.copy, LATE[i])
+        def early_values(first, last):
+            for i in range(first, last + 1):
+                if i < last:
+                    if i + 3 < len(order):
+                        val_raw[order[i + 3]] = load_chunk(values, order[i + 3])
+                    group_values(nc.vector.tensor_copy, EARLY[i])
+                if i > first:
+                    quantise_values(early_packed, len(EARLY), EARLY[i - 1])
 
-        inverse_sum = const.tile([P, HALVES], F32)
-        nc.vector.tensor_reduce(
-            out=inverse_sum[:], in_=anchor_sums[0][:], axis=mybir.AxisListType.X, op=ALU.add
-        )
-        nc.vector.tensor_scalar_add(out=inverse_sum[:], in0=inverse_sum[:], scalar1=1e-8)
-        nc.vector.reciprocal(out=inverse_sum[:], in_=inverse_sum[:])
-        spread_sums = psum_s.tile([P, HALVES, P], F32, tag="bank")
-        for h in range(HALVES):
+        def inverse_row_sums(h):
+            inverse = const.tile([P, 1], F32, name="inverse%d" % h)
+            nc.vector.tensor_reduce(out=inverse[:], in_=anchor_sums[h][:], axis=mybir.AxisListType.X, op=ALU.add)
+            nc.vector.tensor_scalar_add(out=inverse[:], in0=inverse[:], scalar1=1e-8)
+            nc.vector.reciprocal(out=inverse[:], in_=inverse[:])
+            spread_sums = psum_misc.tile([P, P], F32, tag="misc")
             nc.tensor.matmul(
-                out=spread_sums[:, h, :],
-                lhsT=inverse_sum[:, h : h + 1].to_broadcast([P, P]),
-                rhs=identity[:],
-                start=True,
-                stop=True,
+                out=spread_sums[:], lhsT=inverse[:].to_broadcast([P, P]), rhs=identity[:], start=True, stop=True
             )
-        inverse_sums = spread_sums[:].rearrange("p h r -> p (h r)")
-        pool_inverse_sums = const.tile([P, POOL_ROWS], F32)
-        nc.vector.tensor_copy(out=pool_inverse_sums[:], in_=inverse_sums[:, ROWS - POOL_ROWS :])
+            inverses[h] = spread_sums
 
-        quantise_values(packed, 3, LATE[0])
+        def copy_pool_inverses(h):
+            pool_inverses[h] = const.tile([P, POOL_ROWS], F32, name="pool_inverses%d" % h)
+            nc.vector.tensor_copy(out=pool_inverses[h][:], in_=inverses[h][:, VECTOR_ROWS:])
 
-        sums = [psum_s.tile([P, FEATURES], F32, tag="bank", name="sums%d" % h) for h in range(HALVES)]
+        inverses, pool_inverses = {}, {}
 
-        def normalise(c):
-            chunk_grouped = packed.tile([P, ROWS, PACK], BF16, tag="w_grouped", bufs=3, align_bytes=64)
-            vector_rows = ROWS - POOL_ROWS
-            for engine, rows, inverses in (
-                (nc.gpsimd, slice(vector_rows, ROWS), pool_inverse_sums[:]),
-                (nc.vector, slice(0, vector_rows), inverse_sums[:, :vector_rows]),
+        def normalise(c, h):
+            half_grouped = packed.tile([P, P, PACK], BF16, tag="w_grouped", bufs=3, align_bytes=64)
+            for engine, first, last, row_inverses in (
+                (nc.gpsimd, VECTOR_ROWS, P, pool_inverses[h][:]),
+                (nc.vector, 0, VECTOR_ROWS, inverses[h][:, :VECTOR_ROWS]),
             ):
-                pairs = (rows.stop - rows.start) // 2
                 engine.tensor_tensor(
-                    out=chunk_grouped[:, rows, :].rearrange("p (g i) j -> p g j i", i=2),
-                    in0=exps[c][:, :, rows].rearrange("p j (g i) -> p g j i", i=2),
-                    in1=inverses.rearrange("p (g i) -> p g i", i=2).unsqueeze(2).to_broadcast([P, pairs, PACK, 2]),
+                    out=half_grouped[:, first:last, :].rearrange("p (g i) j -> p g j i", i=2),
+                    in0=exps[c][:, :, h * P + first : h * P + last].rearrange("p j (g i) -> p g j i", i=2),
+                    in1=row_inverses.rearrange("p (g i) -> p g i", i=2)
+                    .unsqueeze(2)
+                    .to_broadcast([P, (last - first) // 2, PACK, 2]),
                     op=ALU.mult,
                 )
-            w_grouped[c] = chunk_grouped
+            w_grouped[c, h] = half_grouped
 
-        def quantise_weights(c):
-            codes = packed.tile([P, ROWS], U32, tag="w_codes", align_bytes=64)
-            scales = packed.tile([P, ROWS], U8, tag="w_scales", align_bytes=64)
+        def quantise_weights(c, h, bufs):
+            codes = packed.tile([P, P], U32, tag="w_codes%d" % h, bufs=bufs, align_bytes=64)
+            scales = packed.tile([P, P], U8, tag="w_scales%d" % h, bufs=bufs, align_bytes=64)
             nc.vector.quantize_mx(
                 out=codes[:].bitcast(FP8X4),
                 scales=scales[:],
-                in_=w_grouped[c][:].rearrange("p r j -> p (r j)"),
+                in_=w_grouped[c, h][:].rearrange("p r j -> p (r j)"),
             )
-            w_codes[c], w_scales[c] = codes, scales
+            w_codes[c, h], w_scales[c, h] = codes, scales
 
         def second_passes(c):
             for h in range(HALVES):
                 nc.tensor.matmul_mx(
                     out=sums[h][:],
-                    lhsT=w_codes[c][:, h * P : (h + 1) * P].bitcast(FP8X4),
-                    lhsT_scale=w_scales[c][:, h * P : (h + 1) * P],
+                    lhsT=w_codes[c, h][:].bitcast(FP8X4),
+                    lhsT_scale=w_scales[c, h][:],
                     rhs=val_codes[c][:].bitcast(FP8X4),
                     rhs_scale=val_scales[c][:],
                     start=(c == 0),
                     stop=(c == N_CHUNKS - 1),
                 )
 
+        for c in order[:3]:
+            val_raw[c] = load_chunk(values, c)
+        for c in range(N_CHUNKS):
+            exponential(c, 0)
+            add_to_row_sums(c, 0)
+        early_values(0, N_FIRST)
+        inverse_row_sums(0)
+        early_values(N_FIRST, len(EARLY))
+        copy_pool_inverses(0)
+
+        for c in range(N_CHUNKS):
+            exponential(c, 1)
+            add_to_row_sums(c, 1)
+        for i in range(2):
+            group_values(nc.scalar.copy, LATE[i])
+        for c in range(N_CHUNKS + 1):
+            if c == INVERSES_AT:
+                inverse_row_sums(1)
+            if valid(c):
+                normalise(c, 0)
+            if valid(c - 1):
+                quantise_weights(c - 1, 0, N_CHUNKS)
+            if c in (INVERSES_AT, N_CHUNKS - 1):
+                i = (INVERSES_AT, N_CHUNKS - 1).index(c)
+                quantise_values(packed, 4, LATE[i])
+                val_raw[LATE[i + 3]] = load_chunk(values, LATE[i + 3])
+                group_values(nc.scalar.copy, LATE[i + 2])
+        copy_pool_inverses(1)
+
+        sums = [psum_s.tile([P, FEATURES], F32, tag="bank", name="sums%d" % h) for h in range(HALVES)]
         for c in range(-1, N_CHUNKS):
             if valid(c + 1):
-                normalise(c + 1)
+                normalise(c + 1, 1)
             if valid(c):
-                quantise_weights(c)
+                quantise_weights(c, 1, 3)
             if c in LATE:
                 i = LATE.index(c)
-                if i + 3 < N_LATE:
-                    val_raw[LATE[i + 3]] = load_chunk(values, LATE[i + 3])
+                if i + 5 < N_LATE:
+                    val_raw[LATE[i + 5]] = load_chunk(values, LATE[i + 5])
+                if i + 4 < N_LATE:
+                    group_values(nc.scalar.copy, LATE[i + 4])
                 if i + 2 < N_LATE:
-                    group_values(nc.scalar.copy, LATE[i + 2])
-                if i + 1 < N_LATE:
-                    quantise_values(packed, 3, LATE[i + 1])
+                    quantise_values(packed, 4, LATE[i + 2])
             if valid(c):
                 second_passes(c)
 
-        result_0 = grouped.tile([P, FEATURES], F32, tag="grouped", align_bytes=64)
-        nc.vector.tensor_copy(out=result_0[:], in_=sums[0][:])
-        nc.sync.dma_start(out=out[0], in_=result_0[:])
-        result_1 = grouped.tile([P, FEATURES], F32, tag="grouped", align_bytes=64)
-        nc.scalar.copy(out=result_1[:], in_=sums[1][:])
-        nc.scalar.dma_start(out=out[1], in_=result_1[:])
+        for h, (engine_copy, queue) in enumerate(((nc.vector.tensor_copy, nc.sync), (nc.scalar.copy, nc.scalar))):
+            result = grouped.tile([P, FEATURES], F32, tag="grouped", align_bytes=64)
+            engine_copy(out=result[:], in_=sums[h][:])
+            queue.dma_start(out=out[h], in_=result[:])

@@ -22,6 +22,7 @@ PLANES = WORDS // P
 ANCHORS = 16384
 CHUNK = P * PACK
 N_CHUNKS = ANCHORS // CHUNK
+LEAST = -3.0e38
 POOL_ROWS = 40
 VECTOR_ROWS = P - POOL_ROWS
 N_LATE = 16
@@ -173,7 +174,7 @@ def tile_multiscalegeometricattention_k_kernel(tc, x, positions, values, tempera
         def group_positions(c):
             chunk_grouped = grouped.tile([P, PACK, P, PLANES], F32, tag="grouped", align_bytes=64)
             for pair in range(PACK // 2):
-                on_scalar = c > 2 and pair == 1
+                on_scalar = c > 2 and pair == 1 and c % 4 != 0
                 engine_copy = nc.scalar.copy if on_scalar else nc.vector.tensor_copy
                 engine_copy(
                     out=chunk_grouped[:, 2 * pair : 2 * pair + 2, :, :],
@@ -219,15 +220,11 @@ def tile_multiscalegeometricattention_k_kernel(tc, x, positions, values, tempera
                     op1=ALU.subtract,
                 )
 
-        def arguments(c):
-            for j in range(PACK):
-                nc.vector.tensor_scalar(
-                    out=exps[c][:, j, :],
-                    in0=exps[c][:, j, :],
-                    scalar1=0.0,
-                    scalar2=minus_two_over_tau2[:, c * PACK + j : c * PACK + j + 1],
-                    op0=ALU.min,
-                    op1=ALU.mult,
+        def clamp(c):
+            for pair in range(PACK // 2):
+                blocks = exps[c][:, 2 * pair : 2 * pair + 2, :]
+                nc.gpsimd.tensor_scalar(
+                    out=blocks, in0=blocks, scalar1=0.0, scalar2=LEAST, op0=ALU.min, op1=ALU.max
                 )
 
         def inverse_temperatures():
@@ -246,7 +243,13 @@ def tile_multiscalegeometricattention_k_kernel(tc, x, positions, values, tempera
             nc.scalar.activation(out=magnitude[:], in_=temp_raw[:].rearrange("p c j -> p (c j)"), func=ACT.Abs)
 
         def root(c):
-            nc.scalar.activation(out=exps[c][:], in_=exps[c][:], func=ACT.Sqrt)
+            for j in range(PACK):
+                nc.scalar.activation(
+                    out=exps[c][:, j, :],
+                    in_=exps[c][:, j, :],
+                    func=ACT.Sqrt,
+                    scale=minus_two_over_tau2[:, c * PACK + j : c * PACK + j + 1],
+                )
 
         def half_rows(h):
             return slice(h * P, (h + 1) * P)
@@ -291,6 +294,9 @@ def tile_multiscalegeometricattention_k_kernel(tc, x, positions, values, tempera
                 pos_raw[step + 7] = load_chunk(positions, step + 7)
             if valid(step + 1):
                 first_passes(step + 1)
+            if valid(step):
+                half_distances(step)
+                clamp(step)
             if valid(step + 3):
                 group_positions(step + 3)
             if valid(step + 4):
@@ -300,16 +306,12 @@ def tile_multiscalegeometricattention_k_kernel(tc, x, positions, values, tempera
                 temperature_magnitudes()
             if valid(step + 2):
                 gram(step + 2)
-            if valid(step):
-                half_distances(step)
-            if step == 0:
-                inverse_temperatures()
-            if valid(step):
-                arguments(step)
-            if valid(step + 2):
-                quantise_positions(step + 2)
             if valid(step + 1):
                 gram_norms(step + 1)
+            if step == 0:
+                inverse_temperatures()
+            if valid(step + 2):
+                quantise_positions(step + 2)
             if valid(step - 1):
                 root(step - 1)
 

@@ -23,8 +23,7 @@ ANCHORS = 16384
 CHUNK = P * PACK
 N_CHUNKS = ANCHORS // CHUNK
 LEAST = -3.0e38
-POOL_ROWS = 40
-VECTOR_ROWS = P - POOL_ROWS
+POOL_ROWS = (40, 56)
 N_LATE = 16
 N_FIRST = 12
 INVERSES_AT = N_CHUNKS - 4
@@ -219,13 +218,11 @@ def tile_multiscalegeometricattention_k_kernel(tc, x, positions, values, tempera
                     op0=ALU.subtract,
                     op1=ALU.subtract,
                 )
+            clamp(nc.gpsimd, c, 0)
 
-        def clamp(c):
-            for pair in range(PACK // 2):
-                blocks = exps[c][:, 2 * pair : 2 * pair + 2, :]
-                nc.gpsimd.tensor_scalar(
-                    out=blocks, in0=blocks, scalar1=0.0, scalar2=LEAST, op0=ALU.min, op1=ALU.max
-                )
+        def clamp(engine, c, pair):
+            blocks = exps[c][:, 2 * pair : 2 * pair + 2, :]
+            engine.tensor_scalar(out=blocks, in0=blocks, scalar1=0.0, scalar2=LEAST, op0=ALU.min, op1=ALU.max)
 
         def inverse_temperatures():
             nc.vector.tensor_scalar_add(out=magnitude[:], in0=magnitude[:], scalar1=0.1)
@@ -296,7 +293,6 @@ def tile_multiscalegeometricattention_k_kernel(tc, x, positions, values, tempera
                 first_passes(step + 1)
             if valid(step):
                 half_distances(step)
-                clamp(step)
             if valid(step + 3):
                 group_positions(step + 3)
             if valid(step + 4):
@@ -310,6 +306,8 @@ def tile_multiscalegeometricattention_k_kernel(tc, x, positions, values, tempera
                 gram_norms(step + 1)
             if step == 0:
                 inverse_temperatures()
+            if valid(step):
+                clamp(nc.vector, step, 1)
             if valid(step + 2):
                 quantise_positions(step + 2)
             if valid(step - 1):
@@ -347,16 +345,17 @@ def tile_multiscalegeometricattention_k_kernel(tc, x, positions, values, tempera
             inverses[h] = spread_sums
 
         def copy_pool_inverses(h):
-            pool_inverses[h] = const.tile([P, POOL_ROWS], F32, name="pool_inverses%d" % h)
-            nc.vector.tensor_copy(out=pool_inverses[h][:], in_=inverses[h][:, VECTOR_ROWS:])
+            pool_inverses[h] = const.tile([P, POOL_ROWS[h]], F32, name="pool_inverses%d" % h)
+            nc.vector.tensor_copy(out=pool_inverses[h][:], in_=inverses[h][:, P - POOL_ROWS[h] :])
 
         inverses, pool_inverses = {}, {}
 
         def normalise(c, h):
             half_grouped = packed.tile([P, P, PACK], BF16, tag="w_grouped", bufs=3, align_bytes=64)
+            vector_rows = P - POOL_ROWS[h]
             for engine, first, last, row_inverses in (
-                (nc.gpsimd, VECTOR_ROWS, P, pool_inverses[h][:]),
-                (nc.vector, 0, VECTOR_ROWS, inverses[h][:, :VECTOR_ROWS]),
+                (nc.gpsimd, vector_rows, P, pool_inverses[h][:]),
+                (nc.vector, 0, vector_rows, inverses[h][:, :vector_rows]),
             ):
                 engine.tensor_tensor(
                     out=half_grouped[:, first:last, :].rearrange("p (g i) j -> p g j i", i=2),

@@ -23,7 +23,8 @@ ANCHORS = 16384
 CHUNK = P * PACK
 N_CHUNKS = ANCHORS // CHUNK
 LEAST = -3.0e38
-POOL_ROWS = (40, 56)
+POOL_ROWS = 32
+VECTOR_ROWS = P - POOL_ROWS
 N_LATE = 16
 N_FIRST = 12
 INVERSES_AT = N_CHUNKS - 4
@@ -345,17 +346,16 @@ def tile_multiscalegeometricattention_k_kernel(tc, x, positions, values, tempera
             inverses[h] = spread_sums
 
         def copy_pool_inverses(h):
-            pool_inverses[h] = const.tile([P, POOL_ROWS[h]], F32, name="pool_inverses%d" % h)
-            nc.vector.tensor_copy(out=pool_inverses[h][:], in_=inverses[h][:, P - POOL_ROWS[h] :])
+            pool_inverses[h] = const.tile([P, POOL_ROWS], F32, name="pool_inverses%d" % h)
+            nc.vector.tensor_copy(out=pool_inverses[h][:], in_=inverses[h][:, VECTOR_ROWS:])
 
         inverses, pool_inverses = {}, {}
 
         def normalise(c, h):
             half_grouped = packed.tile([P, P, PACK], BF16, tag="w_grouped", bufs=3, align_bytes=64)
-            vector_rows = P - POOL_ROWS[h]
             for engine, first, last, row_inverses in (
-                (nc.gpsimd, vector_rows, P, pool_inverses[h][:]),
-                (nc.vector, 0, vector_rows, inverses[h][:, :vector_rows]),
+                (nc.gpsimd, VECTOR_ROWS, P, pool_inverses[h][:]),
+                (nc.vector, 0, VECTOR_ROWS, inverses[h][:, :VECTOR_ROWS]),
             ):
                 engine.tensor_tensor(
                     out=half_grouped[:, first:last, :].rearrange("p (g i) j -> p g j i", i=2),

import math
from contextlib import ExitStack

import concourse.mybir as mybir
from concourse.masks import make_identity

F32 = mybir.dt.float32
BF16 = mybir.dt.bfloat16
U32 = mybir.dt.uint32
U8 = mybir.dt.uint8
FP8X4 = mybir.dt.float8_e4m3fn_x4
ALU = mybir.AluOpType
ACT = mybir.ActivationFunctionType

P = 128
PACK = 4
ROWS = 256
HALVES = ROWS // P
FEATURES = 512
WORDS = FEATURES // 2
PLANES = WORDS // P
ANCHORS = 16384
CHUNK = P * PACK
N_CHUNKS = ANCHORS // CHUNK
LEAST = -3.0e38
POOL_ROWS = 32
VECTOR_ROWS = P - POOL_ROWS
N_LATE = 16
N_FIRST = 12
INVERSES_AT = N_CHUNKS - 4
RAW_BUFS = 4

FLOPS = 2 * 2 * ROWS * ANCHORS * FEATURES


def valid(c):
    return 0 <= c < N_CHUNKS


def gram_blocks(c):
    return 1 + c % 2


def is_late(c):
    return c * N_LATE % N_CHUNKS < N_LATE


LATE = [c for c in range(N_CHUNKS) if is_late(c)]
EARLY = [c for c in range(N_CHUNKS) if not is_late(c)]


def transpose_words(nc, bank, rows_bf16, identity):
    words = rows_bf16.bitcast(F32)
    for u in range(PLANES):
        nc.tensor.transpose(bank[:, u, :], words[:, u * P : (u + 1) * P], identity)


def tile_multiscalegeometricattention_k_kernel(tc, x, positions, values, temperature, out):
    nc = tc.nc
    with ExitStack() as stack:
        stack.enter_context(tc.manual_schedule())
        const = stack.enter_context(tc.tile_pool(name="const", bufs=1))
        raw = stack.enter_context(tc.tile_pool(name="raw", bufs=RAW_BUFS))
        grouped = stack.enter_context(tc.tile_pool(name="grouped", bufs=3))
        packed = stack.enter_context(tc.tile_pool(name="packed", bufs=2))
        scratch = stack.enter_context(tc.tile_pool(name="scratch", bufs=4))
        psum_misc = stack.enter_context(tc.psum_pool(name="psum_misc", bufs=2))
        psum_t = stack.enter_context(tc.psum_pool(name="psum_t", bufs=2))
        psum_s = stack.enter_context(tc.psum_pool(name="psum_s", bufs=4))

        identity = const.tile([P, P], F32)
        make_identity(nc, identity[:])

        x_raw = raw.tile([P, HALVES, FEATURES], BF16, tag="chunk_raw")
        nc.sync.dma_start(out=x_raw[:], in_=x.rearrange("h r k -> r h k"))
        x_half_norm = const.tile([P, HALVES], F32)
        for h in range(HALVES):
            squares = scratch.tile([P, FEATURES], BF16, bufs=2)
            nc.scalar.activation(
                out=squares[:],
                in_=x_raw[:, h, :],
                func=ACT.Square,
                scale=math.sqrt(0.5),
                accum_out=x_half_norm[:, h : h + 1],
            )
        x_t = psum_misc.tile([P, HALVES, PLANES, P], F32, tag="misc")
        for h in range(HALVES):
            transpose_words(nc, x_t[:, h, :, :], x_raw[:, h, :], identity[:])
        x_grouped = grouped.tile([P, HALVES, P, PLANES], F32, tag="grouped", align_bytes=64)
        nc.vector.tensor_copy(out=x_grouped[:], in_=x_t[:].rearrange("q h u r -> q h r u"))
        x_codes = const.tile([P, ROWS], U32, align_bytes=64)
        x_scales = const.tile([P, ROWS], U8, align_bytes=64)
        nc.vector.quantize_mx(
            out=x_codes[:].bitcast(FP8X4),
            scales=x_scales[:],
            in_=x_grouped[:].rearrange("q h r u -> q (h r u)").bitcast(BF16),
        )
        spread = psum_misc.tile([P, HALVES, P], F32, tag="misc")
        for h in range(HALVES):
            nc.tensor.matmul(
                out=spread[:, h, :],
                lhsT=x_half_norm[:, h : h + 1].to_broadcast([P, P]),
                rhs=identity[:],
                start=True,
                stop=True,
            )
        x_half_norm_rows = const.tile([P, ROWS], F32)
        nc.vector.tensor_copy(out=x_half_norm_rows[:], in_=spread[:].rearrange("p h r -> p (h r)"))

        exps = [const.tile([P, PACK, ROWS], F32, name="exps%d" % c) for c in range(N_CHUNKS)]
        pos_raw, pos_t, pos_grouped, pos_codes, pos_scales, half_norm, gram_bank, dots = {}, {}, {}, {}, {}, {}, {}, {}
        val_raw, val_grouped, val_codes, val_scales = {}, {}, {}, {}
        w_grouped, w_codes, w_scales = {}, {}, {}
        temp_raw = const.tile([P, N_CHUNKS, PACK], BF16)
        magnitude = const.tile([P, N_CHUNKS * PACK], F32)
        minus_two_over_tau2 = const.tile([P, N_CHUNKS * PACK], F32)

        def load_chunk(source, c):
            chunk_raw = raw.tile([P, PACK, FEATURES], BF16, tag="chunk_raw")
            nc.sync.dma_start(
                out=chunk_raw[:],
                in_=source[c * CHUNK : (c + 1) * CHUNK, :].rearrange("(p j) k -> p j k", j=PACK),
            )
            return chunk_raw

        def transposes(c):
            pos_t[c] = []
            for pair in range(PACK // 2):
                bank = psum_t.tile([P, 2, PLANES, P], F32)
                for b in range(2):
                    transpose_words(nc, bank[:, b, :, :], pos_raw[c][:, 2 * pair + b, :], identity[:])
                pos_t[c].append(bank)

        def norms(c):
            half_norm[c] = [scratch.tile([P, 1], F32, bufs=6 * PACK, name="block_norm") for j in range(PACK)]
            for j in range(gram_blocks(c), PACK):
                squares = scratch.tile([P, FEATURES], BF16, bufs=2)
                nc.scalar.activation(
                    out=squares[:],
                    in_=pos_raw[c][:, j, :],
                    func=ACT.Square,
                    scale=math.sqrt(0.5),
                    accum_out=half_norm[c][j][:],
                )

        def gram(c):
            bank = psum_misc.tile([P, 2, P], F32, tag="misc")
            features = pos_grouped[c][:].rearrange("q j a u -> q (j a u)").bitcast(BF16)
            features = features.rearrange("q (j a t) -> q j a t", j=PACK, t=PACK)
            for j in range(gram_blocks(c)):
                for t in range(PACK):
                    nc.tensor.matmul(
                        out=bank[:, j, :],
                        lhsT=features[:, j, :, t],
                        rhs=features[:, j, :, t],
                        start=(t == 0),
                        stop=(t == PACK - 1),
                    )
            gram_bank[c] = bank

        def gram_norms(c):
            for j in range(gram_blocks(c)):
                diagonal = scratch.tile([P, P], F32, bufs=2)
                nc.vector.scalar_tensor_tensor(
                    out=diagonal[:],
                    in0=gram_bank[c][:, j, :],
                    scalar=0.5,
                    in1=identity[:],
                    op0=ALU.mult,
                    op1=ALU.mult,
                    accum_out=half_norm[c][j][:],
                )

        def group_positions(c):
            chunk_grouped = grouped.tile([P, PACK, P, PLANES], F32, tag="grouped", align_bytes=64)
            for pair in range(PACK // 2):
                on_scalar = c > 2 and pair == 1 and c % 4 != 0
                engine_copy = nc.scalar.copy if on_scalar else nc.vector.tensor_copy
                engine_copy(
                    out=chunk_grouped[:, 2 * pair : 2 * pair + 2, :, :],
                    in_=pos_t[c][pair][:].rearrange("q b u a -> q b a u"),
                )
            pos_grouped[c] = chunk_grouped

        def quantise_positions(c):
            codes = packed.tile([P, CHUNK], U32, tag="codes", bufs=4, align_bytes=64)
            scales = packed.tile([P, CHUNK], U8, tag="scales", bufs=4, align_bytes=64)
            nc.vector.quantize_mx(
                out=codes[:].bitcast(FP8X4),
                scales=scales[:],
                in_=pos_grouped[c][:].rearrange("q j a u -> q (j a u)").bitcast(BF16),
            )
            pos_codes[c], pos_scales[c] = codes, scales

        def first_passes(c):
            dots[c] = []
            for pair in range(PACK // 2):
                bank = psum_s.tile([P, 2, ROWS], F32, tag="bank")
                for b in range(2):
                    j = 2 * pair + b
                    nc.tensor.matmul_mx(
                        out=bank[:, b, :],
                        lhsT=pos_codes[c][:, j * P : (j + 1) * P].bitcast(FP8X4),
                        lhsT_scale=pos_scales[c][:, j * P : (j + 1) * P],
                        rhs=x_codes[:].bitcast(FP8X4),
                        rhs_scale=x_scales[:],
                        start=True,
                        stop=True,
                    )
                dots[c].append(bank)

        def half_distances(c):
            for j in range(PACK):
                nc.vector.scalar_tensor_tensor(
                    out=exps[c][:, j, :],
                    in0=dots[c][j // 2][:, j % 2, :],
                    scalar=half_norm[c][j][:],
                    in1=x_half_norm_rows[:],
                    op0=ALU.subtract,
                    op1=ALU.subtract,
                )
            clamp(nc.gpsimd, c, 0)

        def clamp(engine, c, pair):
            blocks = exps[c][:, 2 * pair : 2 * pair + 2, :]
            engine.tensor_scalar(out=blocks, in0=blocks, scalar1=0.0, scalar2=LEAST, op0=ALU.min, op1=ALU.max)

        def inverse_temperatures():
            nc.vector.tensor_scalar_add(out=magnitude[:], in0=magnitude[:], scalar1=0.1)
            nc.vector.scalar_tensor_tensor(
                out=minus_two_over_tau2[:],
                in0=magnitude[:],
                scalar=-1.0 / 800.0,
                in1=magnitude[:],
                op0=ALU.mult,
                op1=ALU.mult,
            )
            nc.vector.reciprocal(out=minus_two_over_tau2[:], in_=minus_two_over_tau2[:])

        def temperature_magnitudes():
            nc.scalar.activation(out=magnitude[:], in_=temp_raw[:].rearrange("p c j -> p (c j)"), func=ACT.Abs)

        def root(c):
            for j in range(PACK):
                nc.scalar.activation(
                    out=exps[c][:, j, :],
                    in_=exps[c][:, j, :],
                    func=ACT.Sqrt,
                    scale=minus_two_over_tau2[:, c * PACK + j : c * PACK + j + 1],
                )

        def half_rows(h):
            return slice(h * P, (h + 1) * P)

        def exponential(c, h):
            half = exps[c][:, :, half_rows(h)]
            nc.scalar.activation(out=half, in_=half, func=ACT.Exp, scale=-1.0)

        def add_to_row_sums(c, h):
            for j in range(PACK):
                nc.tensor.matmul(
                    out=anchor_sums[h][:],
                    lhsT=exps[c][:, j, half_rows(h)],
                    rhs=identity[:],
                    is_transpose=True,
                    start=(c == 0 and j == 0),
                    stop=(c == N_CHUNKS - 1 and j == PACK - 1),
                )

        def group_values(engine_copy, c):
            chunk_grouped = grouped.tile([P, FEATURES, PACK], BF16, tag="grouped", align_bytes=64)
            engine_copy(
                out=chunk_grouped[:].rearrange("p (g i) j -> p g j i", i=4),
                in_=val_raw[c][:].rearrange("p j (g i) -> p g j i", i=4),
            )
            val_grouped[c] = chunk_grouped

        def quantise_values(pool, bufs, c):
            codes = pool.tile([P, FEATURES], U32, tag="codes", bufs=bufs, align_bytes=64)
            scales = pool.tile([P, FEATURES], U8, tag="scales", bufs=bufs, align_bytes=64)
            nc.vector.quantize_mx(
                out=codes[:].bitcast(FP8X4),
                scales=scales[:],
                in_=val_grouped[c][:].rearrange("p d j -> p (d j)"),
            )
            val_codes[c], val_scales[c] = codes, scales

        early_packed = stack.enter_context(tc.tile_pool(name="early_packed", bufs=1))

        def first_stage_step(step):
            if valid(step + 7):
                pos_raw[step + 7] = load_chunk(positions, step + 7)
            if valid(step + 1):
                first_passes(step + 1)
            if valid(step):
                half_distances(step)
            if valid(step + 3):
                group_positions(step + 3)
            if valid(step + 4):
                transposes(step + 4)
                norms(step + 4)
            if step == -3:
                temperature_magnitudes()
            if valid(step + 2):
                gram(step + 2)
            if valid(step + 1):
                gram_norms(step + 1)
            if step == 0:
                inverse_temperatures()
            if valid(step):
                clamp(nc.vector, step, 1)
            if valid(step + 2):
                quantise_positions(step + 2)
            if valid(step - 1):
                root(step - 1)

        for step in range(-7, N_CHUNKS + 1):
            first_stage_step(step)
            if step == -6:
                with nc.allow_non_contiguous_dma(reason="16,384 values, four to a piece"):
                    nc.sync.dma_start(
                        out=temp_raw[:], in_=temperature.rearrange("(c p j) -> p c j", p=P, j=PACK)
                    )

        anchor_sums = [psum_s.tile([P, P], F32, tag="bank", name="anchor_sums%d" % h) for h in range(HALVES)]
        order = EARLY + LATE

        def early_values(first, last):
            for i in range(first, last + 1):
                if i < last:
                    if i + 3 < len(order):
                        val_raw[order[i + 3]] = load_chunk(values, order[i + 3])
                    group_values(nc.vector.tensor_copy, EARLY[i])
                if i > first:
                    quantise_values(early_packed, len(EARLY), EARLY[i - 1])

        def inverse_row_sums(h):
            inverse = const.tile([P, 1], F32, name="inverse%d" % h)
            nc.vector.tensor_reduce(out=inverse[:], in_=anchor_sums[h][:], axis=mybir.AxisListType.X, op=ALU.add)
            nc.vector.tensor_scalar_add(out=inverse[:], in0=inverse[:], scalar1=1e-8)
            nc.vector.reciprocal(out=inverse[:], in_=inverse[:])
            spread_sums = psum_misc.tile([P, P], F32, tag="misc")
            nc.tensor.matmul(
                out=spread_sums[:], lhsT=inverse[:].to_broadcast([P, P]), rhs=identity[:], start=True, stop=True
            )
            inverses[h] = spread_sums

        def copy_pool_inverses(h):
            pool_inverses[h] = const.tile([P, POOL_ROWS], F32, name="pool_inverses%d" % h)
            nc.vector.tensor_copy(out=pool_inverses[h][:], in_=inverses[h][:, VECTOR_ROWS:])

        inverses, pool_inverses = {}, {}

        def normalise(c, h):
            half_grouped = packed.tile([P, P, PACK], BF16, tag="w_grouped", bufs=3, align_bytes=64)
            for engine, first, last, row_inverses in (
                (nc.gpsimd, VECTOR_ROWS, P, pool_inverses[h][:]),
                (nc.vector, 0, VECTOR_ROWS, inverses[h][:, :VECTOR_ROWS]),
            ):
                engine.tensor_tensor(
                    out=half_grouped[:, first:last, :].rearrange("p (g i) j -> p g j i", i=2),
                    in0=exps[c][:, :, h * P + first : h * P + last].rearrange("p j (g i) -> p g j i", i=2),
                    in1=row_inverses.rearrange("p (g i) -> p g i", i=2)
                    .unsqueeze(2)
                    .to_broadcast([P, (last - first) // 2, PACK, 2]),
                    op=ALU.mult,
                )
            w_grouped[c, h] = half_grouped

        def quantise_weights(c, h, bufs):
            codes = packed.tile([P, P], U32, tag="w_codes%d" % h, bufs=bufs, align_bytes=64)
            scales = packed.tile([P, P], U8, tag="w_scales%d" % h, bufs=bufs, align_bytes=64)
            nc.vector.quantize_mx(
                out=codes[:].bitcast(FP8X4),
                scales=scales[:],
                in_=w_grouped[c, h][:].rearrange("p r j -> p (r j)"),
            )
            w_codes[c, h], w_scales[c, h] = codes, scales

        def second_passes(c):
            for h in range(HALVES):
                nc.tensor.matmul_mx(
                    out=sums[h][:],
                    lhsT=w_codes[c, h][:].bitcast(FP8X4),
                    lhsT_scale=w_scales[c, h][:],
                    rhs=val_codes[c][:].bitcast(FP8X4),
                    rhs_scale=val_scales[c][:],
                    start=(c == 0),
                    stop=(c == N_CHUNKS - 1),
                )

        for c in order[:3]:
            val_raw[c] = load_chunk(values, c)
        for c in range(N_CHUNKS):
            exponential(c, 0)
            add_to_row_sums(c, 0)
        early_values(0, N_FIRST)
        inverse_row_sums(0)
        early_values(N_FIRST, len(EARLY))
        copy_pool_inverses(0)

        for c in range(N_CHUNKS):
            exponential(c, 1)
            add_to_row_sums(c, 1)
        for i in range(2):
            group_values(nc.scalar.copy, LATE[i])
        for c in range(N_CHUNKS + 1):
            if c == INVERSES_AT:
                inverse_row_sums(1)
            if valid(c):
                normalise(c, 0)
            if valid(c - 1):
                quantise_weights(c - 1, 0, N_CHUNKS)
            if c in (INVERSES_AT, N_CHUNKS - 1):
                i = (INVERSES_AT, N_CHUNKS - 1).index(c)
                quantise_values(packed, 4, LATE[i])
                val_raw[LATE[i + 3]] = load_chunk(values, LATE[i + 3])
                group_values(nc.scalar.copy, LATE[i + 2])
        copy_pool_inverses(1)

        sums = [psum_s.tile([P, FEATURES], F32, tag="bank", name="sums%d" % h) for h in range(HALVES)]
        for c in range(-1, N_CHUNKS):
            if valid(c + 1):
                normalise(c + 1, 1)
            if valid(c):
                quantise_weights(c, 1, 3)
            if c in LATE:
                i = LATE.index(c)
                if i + 5 < N_LATE:
                    val_raw[LATE[i + 5]] = load_chunk(values, LATE[i + 5])
                if i + 4 < N_LATE:
                    group_values(nc.scalar.copy, LATE[i + 4])
                if i + 2 < N_LATE:
                    quantise_values(packed, 4, LATE[i + 2])
            if valid(c):
                second_passes(c)

        for h, (engine_copy, queue) in enumerate(((nc.vector.tensor_copy, nc.sync), (nc.scalar.copy, nc.scalar))):
            result = grouped.tile([P, FEATURES], F32, tag="grouped", align_bytes=64)
            engine_copy(out=result[:], in_=sums[h][:])
            queue.dma_start(out=out[h], in_=result[:])
